import numpy as np
import ml_dtypes


def mxq(x, axis, fmt="e4m3"):
    dtype, down = {"e4m3": (ml_dtypes.float8_e4m3fn, 7), "e5m2": (ml_dtypes.float8_e5m2, 14)}[fmt]
    v = np.moveaxis(np.asarray(x, np.float32).astype(ml_dtypes.bfloat16).astype(np.float64), axis, -1)
    blocks = v.reshape(v.shape[:-1] + (-1, 32))
    amax = np.abs(blocks).max(-1, keepdims=True)
    byte = np.maximum(np.where(amax > 0, np.frexp(amax)[1] - 1 + 127, 0) - down, 1)
    scale = np.exp2(byte - 127.0)
    codes = (blocks / scale).astype(np.float32).astype(dtype).astype(np.float64)
    return np.moveaxis((codes * scale).reshape(v.shape), -1, axis)


WIDE = False


def mx_kscale(k):
    if not WIDE:
        return np.ones(k)
    levels = np.array([10, -10, 5, -5, 0])
    a = np.random.permutation(np.resize(levels, k // 512 * 4)).reshape(k // 512, 4)
    idx = np.arange(k)
    return np.exp2(a[idx // 512, idx % 128 // 32])


BF16 = ml_dtypes.bfloat16


def bf(x):
    return np.asarray(x, np.float32).astype(BF16)


def f64(x):
    return np.asarray(x).astype(np.float64)


B, T, C, F = 8, 1024, 1024, 512
M = T


def silu(v):
    return v / (1.0 + np.exp(-v))


def sigmoid(v):
    return 1.0 / (1.0 + np.exp(-v))


def setup_inputs():
    t = mx_kscale(F)
    x = np.random.standard_normal((B, T, C)) + 0.5 * np.random.standard_normal((B, 1, C))
    return {"h": bf(silu(np.random.standard_normal((B, T, F)) * 0.85) * t),
            "x": bf(x),
            "memory": bf(np.random.standard_normal((1, M, C)) * 6.0 / np.sqrt(C)),
            "w2": bf(np.random.standard_normal((F, C)) * 3.0 / np.sqrt(F) / t[:, None]),
            "b2": bf(np.random.standard_normal(C) * 0.5)}


def reference(h, x, memory, w2, b2):
    update_gate = sigmoid((mxq(f64(h), 2, "e4m3") @ mxq(f64(w2), 0, "e4m3")) + f64(b2))
    x_mean = f64(x).mean(axis=1, keepdims=True)
    new_mem = f64(memory) * (1.0 - update_gate) + x_mean * update_gate
    return new_mem.mean(axis=0, keepdims=True)

@@ -1,0 +1,464 @@
+from contextlib import ExitStack
+
+import concourse.bass as bass
+import concourse.mybir as mybir
+import concourse.tile as tile
+from concourse.masks import make_identity
+
+F32 = mybir.dt.float32
+BF16 = mybir.dt.bfloat16
+U32 = mybir.dt.uint32
+U8 = mybir.dt.uint8
+FP8X4 = mybir.dt.float8_e4m3fn_x4
+ALU = mybir.AluOpType
+ACT = mybir.ActivationFunctionType
+
+P = 128
+NB = 8
+NT = 1024
+NC = 1024
+NK = 512
+MCH = 512
+FLOPS = 2 * NB * NT * NK * NC
+
+MANUAL = True
+G_BUFS = 26
+ACC_BUFS = 7
+TQ_BUFS = 6
+X_BUFS = 4
+H_BUFS = 8
+REL = {0: [6, 7, 8, 9, 10, 12, 14, 16], 1: [17, 18, 19, 20, 21, 22, 23, 24]}
+XA_FIRST = 5
+PREP1 = [14, 15, 16, 17, 18, 19, 20, 21]
+T2_PER_STEP = 1
+T2_LAG = 2
+W2_STEP = 7
+S2_MAX = 6
+HEAD_ON_SCALAR = True
+DIRECT = {13: [7], 14: [6, 7], 15: [5, 6, 7]}
+S1_ON_VECTOR = [0, 1]
+
+
+def tile_dynamicmemorybank_pb_t_kernel(tc, h, x, memory, w2, b2, out):
+    nc = tc.nc
+    with ExitStack() as ctx:
+        const = ctx.enter_context(tc.tile_pool(name="const", bufs=1))
+        hstage = ctx.enter_context(tc.tile_pool(name="hstage", bufs=H_BUFS))
+        xstage = ctx.enter_context(tc.tile_pool(name="xstage", bufs=X_BUFS))
+        grpp = ctx.enter_context(tc.tile_pool(name="grp", bufs=6))
+        gp = ctx.enter_context(tc.tile_pool(name="g", bufs=G_BUFS))
+        accp = ctx.enter_context(tc.tile_pool(name="acc", bufs=ACC_BUFS))
+        tqp = ctx.enter_context(tc.tile_pool(name="tq", bufs=TQ_BUFS))
+        otp = ctx.enter_context(tc.tile_pool(name="ot", bufs=3))
+        zp = ctx.enter_context(tc.psum_pool(name="z", bufs=4))
+        auxp = ctx.enter_context(tc.psum_pool(name="aux", bufs=4))
+        if MANUAL:
+            ctx.enter_context(tc.manual_schedule())
+
+        ident = const.tile([P, P], F32, name="ident")
+        make_identity(nc, ident[:])
+        ones = const.tile([P, 2], BF16, name="ones")
+        nc.vector.memset(ones[:], 1.0 / 8192.0)
+        warm = const.tile([P, 1], F32, name="warm")
+        nc.vector.memset(warm[:], 0.0)
+        nc.scalar.activation(out=warm[:], in_=warm[:], func=ACT.Sigmoid)
+        bzf = const.tile([P, P], F32, name="bzf")
+        nc.vector.memset(bzf[:], 0.0)
+
+        w2raw = xstage.tile([P, 4096], BF16, tag="xs", name="w2raw")
+        for u in range(2):
+            nc.sync.dma_start(
+                out=w2raw[:, u * 2048 : (u + 1) * 2048],
+                in_=w2[u * 256 : (u + 1) * 256, :].rearrange("(q e) c -> q (e c)", e=2),
+            )
+        b2r = const.tile([8, P], BF16, name="b2r")
+        nc.sync.dma_start(out=b2r[:], in_=b2.rearrange("(r c) -> r c", c=P))
+
+        hs = {}
+        xs = {}
+        mem = {}
+
+        def load_h(b, mc):
+            t = hstage.tile([P, 2048], BF16, tag="hs", name="hs")
+            nc.sync.dma_start(
+                out=t[:],
+                in_=h[b, mc * MCH : (mc + 1) * MCH, :].rearrange("(p t) k -> p (t k)", t=4),
+            )
+            hs[(b, mc)] = t
+
+        def load_mem(mc):
+            t = const.tile([P, 4096], BF16, name="mem%d" % mc)
+            nc.sync.dma_start(
+                out=t[:],
+                in_=memory[0, mc * MCH : (mc + 1) * MCH, :].rearrange("(p t) c -> p (t c)", t=4),
+            )
+            mem[mc] = t
+
+        def load_x(b, ch):
+            t = xstage.tile([P, 4096], BF16, tag="xs", name="xs")
+            nc.sync.dma_start(
+                out=t[:].rearrange("p (r c) -> p r c", r=8),
+                in_=x[b, :, ch * 512 : (ch + 1) * 512].rearrange("(p r) c -> p r c", r=8),
+            )
+            xs[(b, ch)] = t
+
+        loadq = [("h", b, 0) for b in range(NB)] + [("m", 0, 0)]
+        loadq += [("x", b, 0) for b in range(XA_FIRST)]
+        for i in range(4):
+            loadq += [("h", 2 * i, 1), ("h", 2 * i + 1, 1)]
+            if XA_FIRST + i < NB:
+                loadq += [("x", XA_FIRST + i, 0)]
+        loadq += [("m", 1, 0)] + [("x", b, 1) for b in range(NB)]
+        st = {"next": 0, "x": 1, "h": 0}
+
+        def pump():
+            while st["next"] < len(loadq):
+                kind, a0, a1 = loadq[st["next"]]
+                if kind == "x" and st["x"] >= X_BUFS:
+                    return
+                if kind == "h" and st["h"] >= H_BUFS:
+                    return
+                if kind == "x":
+                    load_x(a0, a1)
+                    st["x"] += 1
+                elif kind == "h":
+                    load_h(a0, a1)
+                    st["h"] += 1
+                else:
+                    load_mem(a0)
+                st["next"] += 1
+
+        pump()
+
+        w2c = [const.tile([P, 512], U32, name="w2c%d" % i, align_bytes=64) for i in range(2)]
+        w2s = [const.tile([P, 512], U8, name="w2s%d" % i, align_bytes=64) for i in range(2)]
+        w2v = w2raw[:].rearrange("p (t c) -> p c t", t=4)
+
+        def w2_regroup(q, eng):
+            gw = grpp.tile([P, 1024], BF16, tag="grp", name="gw", align_bytes=64)
+            dst = gw[:].rearrange("p (c t) -> p c t", t=4)
+            src = w2v[:, q * 256 : (q + 1) * 256, :]
+            if eng == "v":
+                nc.vector.tensor_copy(out=dst, in_=src)
+            else:
+                nc.scalar.copy(out=dst, in_=src)
+            return gw
+
+        def w2_quant(q, gw):
+            nc.vector.quantize_mx(
+                out=w2c[q // 2][:, (q % 2) * 256 : (q % 2 + 1) * 256].bitcast(FP8X4),
+                scales=w2s[q // 2][:, (q % 2) * 256 : (q % 2 + 1) * 256],
+                in_=gw[:],
+            )
+
+        hc = {}
+        hsc = {}
+
+        def prep_h_front(b, mc, engines, pool, tag):
+            hc[(b, mc)] = const.tile([P, MCH], U32, name="hc%d_%d" % (b, mc), align_bytes=64)
+            hsc[(b, mc)] = const.tile([P, MCH], U8, name="hsc%d_%d" % (b, mc), align_bytes=64)
+            hw = hs[(b, mc)][:].bitcast(F32)
+            pend = []
+            for half in range(2):
+                xt = pool.tile([P, 512], F32, tag=tag, name="xt")
+                for ttl in range(2):
+                    tt = 2 * half + ttl
+                    for u in range(2):
+                        nc.tensor.transpose(
+                            xt[:, u * 256 + ttl * P : u * 256 + (ttl + 1) * P],
+                            hw[:, tt * 256 + u * P : tt * 256 + (u + 1) * P],
+                            ident[:],
+                        )
+                gh = grpp.tile([P, 1024], BF16, tag="grp", name="gh", align_bytes=64)
+                dst = gh[:].bitcast(F32).rearrange("p (c u) -> p c u", u=2)
+                src = xt[:].rearrange("p (u c) -> p c u", u=2)
+                if engines[half] == "v":
+                    nc.vector.tensor_copy(out=dst, in_=src)
+                else:
+                    nc.scalar.copy(out=dst, in_=src)
+                pend.append((b, mc, half, gh))
+            st["h"] -= 1
+            pump()
+            return pend
+
+        def prep_h_back(pend):
+            for b, mc, half, gh in pend:
+                nc.vector.quantize_mx(
+                    out=hc[(b, mc)][:, half * 256 : (half + 1) * 256].bitcast(FP8X4),
+                    scales=hsc[(b, mc)][:, half * 256 : (half + 1) * 256],
+                    in_=gh[:],
+                )
+
+        units = [(mc, ct) for ch in range(2) for mc in range(2) for ct in range(4 * ch, 4 * ch + 4)]
+        NU = len(units)
+        gt = {}
+        s1 = {}
+        accs = {}
+        ndone = {}
+        tqs = {}
+        U = {}
+
+        def mx_sig(tiles):
+            zs = []
+            for j, b in tiles:
+                mc, ct = units[j]
+                z = zp.tile([P, 512], F32, tag="z", name="z")
+                nc.tensor.matmul_mx(
+                    out=z[:],
+                    lhsT=w2c[ct // 4][:, (ct % 4) * P : (ct % 4 + 1) * P].bitcast(FP8X4),
+                    lhsT_scale=w2s[ct // 4][:, (ct % 4) * P : (ct % 4 + 1) * P],
+                    rhs=hc[(b, mc)][:].bitcast(FP8X4),
+                    rhs_scale=hsc[(b, mc)][:],
+                    start=True,
+                    stop=True,
+                )
+                zs.append(z)
+            for jb, z in zip(tiles, zs):
+                ct = units[jb[0]][1]
+                g = gp.tile([P, 512], F32, tag="g", name="g")
+                nc.scalar.activation(
+                    out=g[:], in_=z[:], func=ACT.Sigmoid, bias=b2T[:, ct : ct + 1], scale=1.0
+                )
+                gt[jb] = g
+
+        a1 = {}
+
+        def s1_vec(j, b):
+            g = gt[(j, b)]
+            if b == 0:
+                return
+            if b == 1:
+                a1[j] = accp.tile([P, 512], F32, tag="acc", name="a1")
+                nc.vector.tensor_tensor(out=a1[j][:], in0=gt[(j, 0)][:], in1=g[:], op=ALU.add)
+            else:
+                nc.vector.tensor_tensor(out=a1[j][:], in0=a1[j][:], in1=g[:], op=ALU.add)
+
+        def s1_vec_pe(j):
+            s1[j] = auxp.tile([P, 512], F32, tag="aux", name="s1")
+            for tt in range(4):
+                nc.tensor.transpose(
+                    s1[j][:, tt * P : (tt + 1) * P], a1[j][:, tt * P : (tt + 1) * P], ident[:]
+                )
+
+        def s1_add(tiles):
+            for j, b in tiles:
+                if j in S1_ON_VECTOR:
+                    continue
+                if b == 0:
+                    s1[j] = auxp.tile([P, 512], F32, tag="aux", name="s1")
+                g = gt[(j, b)]
+                for tt in range(4):
+                    nc.tensor.matmul(
+                        out=s1[j][:, tt * P : (tt + 1) * P],
+                        lhsT=g[:, tt * P : (tt + 1) * P],
+                        rhs=ident[:],
+                        is_transpose=True,
+                        start=(b == 0 and tt == 0),
+                        stop=(b == NB - 1 and tt == 3),
+                    )
+
+        def s2_add(j, b):
+            mc, ct = units[j]
+            g = gt[(j, b)]
+            n = ndone.get(j, 0)
+            sc = U[(b, ct // 4)][:, ct % 4 : ct % 4 + 1]
+            if n == 0:
+                a = accp.tile([P, 512], F32, tag="acc", name="acc")
+                accs[j] = a
+                if HEAD_ON_SCALAR:
+                    nc.scalar.activation(out=a[:], in_=g[:], func=ACT.Copy, scale=sc)
+                else:
+                    nc.vector.tensor_scalar(out=a[:], in0=g[:], scalar1=sc, scalar2=None, op0=ALU.mult)
+            else:
+                a = accs[j]
+                nc.vector.scalar_tensor_tensor(
+                    out=a[:], in0=g[:], scalar=sc, in1=a[:], op0=ALU.mult, op1=ALU.add
+                )
+            ndone[j] = n + 1
+
+        def fin1(j):
+            mc, ct = units[j]
+            tq = tqp.tile([P, 512], F32, tag="tq", name="tq")
+            nc.vector.scalar_tensor_tensor(
+                out=tq[:].rearrange("p (t c) -> p t c", t=4),
+                in0=s1[j][:].rearrange("p (t c) -> p t c", t=4),
+                scalar=8.0,
+                in1=mem[mc][:].rearrange("p (t c) -> p t c", t=4)[:, :, ct * P : (ct + 1) * P],
+                op0=ALU.subtract,
+                op1=ALU.mult,
+            )
+            tqs[j] = tq
+
+        t2s = {}
+        sgs = {}
+
+        def direct_scale(j, b):
+            ct = units[j][1]
+            sg = gp.tile([P, 512], F32, tag="g", name="sg")
+            nc.scalar.activation(
+                out=sg[:], in_=gt[(j, b)][:], func=ACT.Copy, scale=U[(b, ct // 4)][:, ct % 4 : ct % 4 + 1]
+            )
+            sgs[(j, b)] = sg
+
+        def t2_part(j, src, first, last):
+            if first:
+                t2s[j] = auxp.tile([P, 512], F32, tag="aux", name="t2")
+            for tt in range(4):
+                nc.tensor.matmul(
+                    out=t2s[j][:, tt * P : (tt + 1) * P],
+                    lhsT=src[:, tt * P : (tt + 1) * P],
+                    rhs=ident[:],
+                    is_transpose=True,
+                    start=(first and tt == 0),
+                    stop=(last and tt == 3),
+                )
+
+        def t2_pe(j):
+            ds = DIRECT.get(j, [])
+            for i, b in enumerate(ds):
+                t2_part(j, sgs[(j, b)], i == 0, False)
+            t2_part(j, accs[j], len(ds) == 0, True)
+
+        def fin2(j):
+            mc, ct = units[j]
+            ot = otp.tile([P, 512], F32, tag="ot", name="ot")
+            nc.vector.scalar_tensor_tensor(
+                out=ot[:], in0=tqs[j][:], scalar=-0.125, in1=t2s[j][:], op0=ALU.mult, op1=ALU.add
+            )
+            nc.sync.dma_start(
+                out=out[0, mc * MCH : (mc + 1) * MCH, ct * P : (ct + 1) * P].rearrange(
+                    "(p t) c -> p t c", t=4
+                ),
+                in_=ot[:].rearrange("p (t c) -> p t c", t=4),
+            )
+
+        xps = {}
+
+        def xmean_pe(b, ch):
+            ps = auxp.tile([P, 512], F32, tag="aux", name="xps")
+            for c4 in range(4):
+                for r in range(8):
+                    nc.tensor.matmul(
+                        out=ps[:, c4 * 2 : c4 * 2 + 2],
+                        lhsT=xs[(b, ch)][:, r * 512 + c4 * P : r * 512 + (c4 + 1) * P],
+                        rhs=ones[:],
+                        start=(r == 0),
+                        stop=(r == 7),
+                    )
+            xps[(b, ch)] = ps
+            st["x"] -= 1
+            pump()
+
+        def xmean_out(b, ch):
+            ub = const.tile([P, 4], F32, name="U%d_%d" % (b, ch))
+            nc.vector.tensor_copy(
+                out=ub[:], in_=xps[(b, ch)][:, 0:8].rearrange("p (c two) -> p c two", two=2)[:, :, 0]
+            )
+            U[(b, ch)] = ub
+
+        gw0 = w2_regroup(0, "v")
+        gw1 = w2_regroup(1, "s")
+        nc.vector.tensor_copy(out=bzf[0:8, :], in_=b2r[:])
+        b2ps = auxp.tile([P, 512], F32, tag="aux", name="b2ps")
+        nc.tensor.transpose(b2ps[:, 0:P], bzf[:], ident[:])
+        b2T = const.tile([P, 8], F32, name="b2T")
+        w2_quant(0, gw0)
+        nc.vector.tensor_copy(out=b2T[:], in_=b2ps[:, 0:8])
+        w2_quant(1, gw1)
+        pend = prep_h_front(0, 0, ("v", "s"), zp, "z")
+        new = prep_h_front(1, 0, ("v", "s"), zp, "z")
+        prep_h_back(pend)
+        prep_h_back(new)
+        pend = []
+
+        rounds = []
+        prep_at = {}
+        for j in range(0, NU, 2):
+            if j in (0, 4):
+                for b in range(NB):
+                    if len(rounds) + b - 2 >= 0:
+                        prep_at[len(rounds) + b - 2] = (b, j // 4)
+                rounds += [[(j, b), (j + 1, b)] for b in range(NB)]
+            else:
+                for jj in (j, j + 1):
+                    rounds.append([(jj, b) for b in range(4)])
+                    rounds.append([(jj, b) for b in range(4, 8)])
+        NR = len(rounds)
+        t2_wait = []
+        fin2_wait = []
+        made = []
+        released = []
+
+        t2_age = {}
+        s1v_pe = []
+        s1v_wait = []
+        for r in range(NR + 8):
+            if r < NR:
+                mx_sig(rounds[r])
+            new = []
+            if 1 <= r <= NR:
+                s1_add(rounds[r - 1])
+            newly = [(b, ch) for ch in range(2) for b in range(NB) if REL[ch][b] == r]
+            for b, ch in newly:
+                xmean_pe(b, ch)
+            for j in s1v_pe:
+                s1_vec_pe(j)
+                s1v_wait.append(j)
+            s1v_pe = []
+            now_t2 = [j for j in t2_wait if t2_age[j] + T2_LAG <= r][:T2_PER_STEP]
+            t2_wait = [j for j in t2_wait if j not in now_t2]
+            for j in now_t2:
+                t2_pe(j)
+            if r in prep_at:
+                new.extend(
+                    prep_h_front(prep_at[r][0], prep_at[r][1], ("v" if r < 8 else "s", "s"), auxp, "aux")
+                )
+            for j in s1v_wait:
+                fin1(j)
+            s1v_wait = []
+            if 1 <= r <= NR:
+                for j, b in rounds[r - 1]:
+                    if j in S1_ON_VECTOR:
+                        s1_vec(j, b)
+                        if b == NB - 1:
+                            s1v_pe.append(j)
+                    elif b == NB - 1:
+                        fin1(j)
+                    if b in DIRECT.get(j, []):
+                        direct_scale(j, b)
+                    else:
+                        made.append((j, b))
+            for b, ch in newly:
+                xmean_out(b, ch)
+                released.append((b, ch))
+            for j in fin2_wait:
+                fin2(j)
+            fin2_wait = now_t2
+            prep_h_back(new)
+            if r == W2_STEP:
+                gw2 = w2_regroup(2, "s")
+                gw3 = w2_regroup(3, "s")
+                st["x"] -= 1
+                pump()
+                w2_quant(2, gw2)
+                w2_quant(3, gw3)
+            ready = [jb for jb in made if (jb[1], units[jb[0]][1] // 4) in released]
+            quota = min(S2_MAX, max(0, len(ready) - 4))
+            if r >= NR - 4:
+                quota = 8
+            taken = []
+            while ready and len(taken) < quota:
+                seen = []
+                rest = []
+                for jb in ready:
+                    if jb[0] in seen or len(taken) >= quota:
+                        rest.append(jb)
+                    else:
+                        seen.append(jb[0])
+                        taken.append(jb)
+                        s2_add(jb[0], jb[1])
+                        if ndone[jb[0]] == NB - len(DIRECT.get(jb[0], [])):
+                            t2_wait.append(jb[0])
+                            t2_age[jb[0]] = r
+                ready = rest
+            made = [jb for jb in made if jb not in taken]

@@ -96,10 +96,10 @@ def tile_dynamicmemorybank_pb_t_kernel(tc, h, x, memory, w2, b2, out):
 
         def load_x(b, ch):
             t = xstage.tile([P, 4096], BF16, tag="xs", name="xs")
-            nc.sync.dma_start(
-                out=t[:].rearrange("p (r c) -> p r c", r=8),
-                in_=x[b, :, ch * 512 : (ch + 1) * 512].rearrange("(p r) c -> p r c", r=8),
-            )
+            xv = x[b, :, ch * 512 : (ch + 1) * 512].rearrange("(p r) c -> p r c", r=8)
+            tv = t[:].rearrange("p (r c) -> p r c", r=8)
+            for i in range(2):
+                nc.sync.dma_start(out=tv[:, 4 * i : 4 * i + 4, :], in_=xv[:, 4 * i : 4 * i + 4, :])
             xs[(b, ch)] = t
 
         loadq = [("h", b, 0) for b in range(NB)] + [("m", 0, 0)]

@@ -22,21 +22,27 @@ MCH = 512
 FLOPS = 2 * NB * NT * NK * NC
 
 MANUAL = True
+Z_BUFS = 0
+GRP_BUFS = 8
+LEAD = 3
+MC1_COPY = "ss"
+XOUT_LAG = 1
+FIN1_LAG = 1
 G_BUFS = 26
 ACC_BUFS = 7
 TQ_BUFS = 6
 X_BUFS = 4
 H_BUFS = 8
-REL = {0: [6, 7, 8, 9, 10, 12, 14, 16], 1: [17, 18, 19, 20, 21, 22, 23, 24]}
+REL = [[6, 7, 8, 9, 10, 12, 14, 16], [17, 18, 19, 20, 21, 22, 23, 24]]
 XA_FIRST = 5
 PREP1 = [14, 15, 16, 17, 18, 19, 20, 21]
 T2_PER_STEP = 1
 T2_LAG = 2
-W2_STEP = 7
+W2_STEP = 9
 S2_MAX = 6
-HEAD_ON_SCALAR = True
+HEAD_ON_SCALAR = False
 DIRECT = {13: [7], 14: [6, 7], 15: [5, 6, 7]}
-S1_ON_VECTOR = [0, 1]
+S1_ON_VECTOR = [1]
 
 
 def tile_dynamicmemorybank_pb_t_kernel(tc, h, x, memory, w2, b2, out):
@@ -45,13 +51,13 @@ def tile_dynamicmemorybank_pb_t_kernel(tc, h, x, memory, w2, b2, out):
         const = ctx.enter_context(tc.tile_pool(name="const", bufs=1))
         hstage = ctx.enter_context(tc.tile_pool(name="hstage", bufs=H_BUFS))
         xstage = ctx.enter_context(tc.tile_pool(name="xstage", bufs=X_BUFS))
-        grpp = ctx.enter_context(tc.tile_pool(name="grp", bufs=6))
+        grpp = ctx.enter_context(tc.tile_pool(name="grp", bufs=GRP_BUFS))
         gp = ctx.enter_context(tc.tile_pool(name="g", bufs=G_BUFS))
         accp = ctx.enter_context(tc.tile_pool(name="acc", bufs=ACC_BUFS))
         tqp = ctx.enter_context(tc.tile_pool(name="tq", bufs=TQ_BUFS))
         otp = ctx.enter_context(tc.tile_pool(name="ot", bufs=3))
-        zp = ctx.enter_context(tc.psum_pool(name="z", bufs=4))
-        auxp = ctx.enter_context(tc.psum_pool(name="aux", bufs=4))
+        zp = ctx.enter_context(tc.psum_pool(name="z", bufs=Z_BUFS)) if Z_BUFS > 0 else None
+        auxp = ctx.enter_context(tc.psum_pool(name="aux", bufs=8 - Z_BUFS))
         if MANUAL:
             ctx.enter_context(tc.manual_schedule())
 
@@ -154,13 +160,13 @@ def tile_dynamicmemorybank_pb_t_kernel(tc, h, x, memory, w2, b2, out):
         hc = {}
         hsc = {}
 
-        def prep_h_front(b, mc, engines, pool, tag):
+        def prep_pe(b, mc):
             hc[(b, mc)] = const.tile([P, MCH], U32, name="hc%d_%d" % (b, mc), align_bytes=64)
             hsc[(b, mc)] = const.tile([P, MCH], U8, name="hsc%d_%d" % (b, mc), align_bytes=64)
             hw = hs[(b, mc)][:].bitcast(F32)
-            pend = []
+            xts = []
             for half in range(2):
-                xt = pool.tile([P, 512], F32, tag=tag, name="xt")
+                xt = auxp.tile([P, 512], F32, tag="aux", name="xt")
                 for ttl in range(2):
                     tt = 2 * half + ttl
                     for u in range(2):
@@ -169,17 +175,21 @@ def tile_dynamicmemorybank_pb_t_kernel(tc, h, x, memory, w2, b2, out):
                             hw[:, tt * 256 + u * P : tt * 256 + (u + 1) * P],
                             ident[:],
                         )
-                gh = grpp.tile([P, 1024], BF16, tag="grp", name="gh", align_bytes=64)
-                dst = gh[:].bitcast(F32).rearrange("p (c u) -> p c u", u=2)
-                src = xt[:].rearrange("p (u c) -> p c u", u=2)
-                if engines[half] == "v":
-                    nc.vector.tensor_copy(out=dst, in_=src)
-                else:
-                    nc.scalar.copy(out=dst, in_=src)
-                pend.append((b, mc, half, gh))
+                xts.append(xt)
             st["h"] -= 1
             pump()
-            return pend
+            return (b, mc, xts)
+
+        def prep_copy(job, half, eng):
+            b, mc, xts = job
+            gh = grpp.tile([P, 1024], BF16, tag="grp", name="gh", align_bytes=64)
+            dst = gh[:].bitcast(F32).rearrange("p (c u) -> p c u", u=2)
+            src = xts[half][:].rearrange("p (u c) -> p c u", u=2)
+            if eng == "v":
+                nc.vector.tensor_copy(out=dst, in_=src)
+            else:
+                nc.scalar.copy(out=dst, in_=src)
+            return (b, mc, half, gh)
 
         def prep_h_back(pend):
             for b, mc, half, gh in pend:
@@ -200,9 +210,13 @@ def tile_dynamicmemorybank_pb_t_kernel(tc, h, x, memory, w2, b2, out):
 
         def mx_sig(tiles):
             zs = []
-            for j, b in tiles:
+            for i, jb in enumerate(tiles):
+                j, b = jb
                 mc, ct = units[j]
-                z = zp.tile([P, 512], F32, tag="z", name="z")
+                if i < Z_BUFS:
+                    z = zp.tile([P, 512], F32, tag="z", name="z")
+                else:
+                    z = auxp.tile([P, 512], F32, tag="aux", name="z")
                 nc.tensor.matmul_mx(
                     out=z[:],
                     lhsT=w2c[ct // 4][:, (ct % 4) * P : (ct % 4 + 1) * P].bitcast(FP8X4),
@@ -365,19 +379,13 @@ def tile_dynamicmemorybank_pb_t_kernel(tc, h, x, memory, w2, b2, out):
         w2_quant(0, gw0)
         nc.vector.tensor_copy(out=b2T[:], in_=b2ps[:, 0:8])
         w2_quant(1, gw1)
-        pend = prep_h_front(0, 0, ("v", "s"), zp, "z")
-        new = prep_h_front(1, 0, ("v", "s"), zp, "z")
-        prep_h_back(pend)
-        prep_h_back(new)
-        pend = []
 
         rounds = []
         prep_at = {}
         for j in range(0, NU, 2):
             if j in (0, 4):
                 for b in range(NB):
-                    if len(rounds) + b - 2 >= 0:
-                        prep_at[len(rounds) + b - 2] = (b, j // 4)
+                    prep_at[len(rounds) + b - LEAD] = (b, j // 4)
                 rounds += [[(j, b), (j + 1, b)] for b in range(NB)]
             else:
                 for jj in (j, j + 1):
@@ -385,77 +393,97 @@ def tile_dynamicmemorybank_pb_t_kernel(tc, h, x, memory, w2, b2, out):
                     rounds.append([(jj, b) for b in range(4, 8)])
         NR = len(rounds)
         t2_wait = []
+        t2_age = {}
         fin2_wait = []
+        fin1_wait = []
+        xout_wait = []
         made = []
         released = []
-
-        t2_age = {}
         s1v_pe = []
-        s1v_wait = []
-        for r in range(NR + 8):
-            if r < NR:
+        copy_wait = []
+        quant_wait = []
+
+        for r in range(-LEAD, NR + 8):
+            if 0 <= r < NR:
                 mx_sig(rounds[r])
-            new = []
+            for ch in range(2):
+                for b in range(NB):
+                    if REL[ch][b] == r:
+                        xmean_pe(b, ch)
+                        xout_wait.append((r, b, ch))
             if 1 <= r <= NR:
                 s1_add(rounds[r - 1])
-            newly = [(b, ch) for ch in range(2) for b in range(NB) if REL[ch][b] == r]
-            for b, ch in newly:
-                xmean_pe(b, ch)
+                for j, b in rounds[r - 1]:
+                    if b == NB - 1 and j not in S1_ON_VECTOR:
+                        fin1_wait.append((r, j))
             for j in s1v_pe:
                 s1_vec_pe(j)
-                s1v_wait.append(j)
+                fin1_wait.append((r, j))
             s1v_pe = []
             now_t2 = [j for j in t2_wait if t2_age[j] + T2_LAG <= r][:T2_PER_STEP]
             t2_wait = [j for j in t2_wait if j not in now_t2]
             for j in now_t2:
                 t2_pe(j)
+            new_copy = []
             if r in prep_at:
-                new.extend(
-                    prep_h_front(prep_at[r][0], prep_at[r][1], ("v" if r < 8 else "s", "s"), auxp, "aux")
-                )
-            for j in s1v_wait:
-                fin1(j)
-            s1v_wait = []
+                new_copy.append(prep_pe(prep_at[r][0], prep_at[r][1]))
+            new_quant = []
+            for job in copy_wait:
+                engs = "vs" if job[1] == 0 else MC1_COPY
+                new_quant.append(prep_copy(job, 0, engs[0]))
+                new_quant.append(prep_copy(job, 1, engs[1]))
+            copy_wait = new_copy
+            for rr, j in fin1_wait:
+                if rr + FIN1_LAG <= r:
+                    fin1(j)
+            fin1_wait = [e for e in fin1_wait if e[0] + FIN1_LAG > r]
+            for rr, b, ch in xout_wait:
+                if rr + XOUT_LAG <= r:
+                    xmean_out(b, ch)
+                    released.append((b, ch))
+            xout_wait = [e for e in xout_wait if e[0] + XOUT_LAG > r]
+            for j in fin2_wait:
+                fin2(j)
+            fin2_wait = now_t2
+            prep_h_back(quant_wait)
+            quant_wait = new_quant
+            if r == W2_STEP:
+                gw2 = w2_regroup(2, "s")
+                gw3 = w2_regroup(3, "s")
+                st["x"] -= 1
+                pump()
+            if r == W2_STEP + 1:
+                w2_quant(2, gw2)
+                w2_quant(3, gw3)
             if 1 <= r <= NR:
                 for j, b in rounds[r - 1]:
                     if j in S1_ON_VECTOR:
                         s1_vec(j, b)
                         if b == NB - 1:
                             s1v_pe.append(j)
-                    elif b == NB - 1:
-                        fin1(j)
                     if b in DIRECT.get(j, []):
                         direct_scale(j, b)
                     else:
                         made.append((j, b))
-            for b, ch in newly:
-                xmean_out(b, ch)
-                released.append((b, ch))
-            for j in fin2_wait:
-                fin2(j)
-            fin2_wait = now_t2
-            prep_h_back(new)
-            if r == W2_STEP:
-                gw2 = w2_regroup(2, "s")
-                gw3 = w2_regroup(3, "s")
-                st["x"] -= 1
-                pump()
-                w2_quant(2, gw2)
-                w2_quant(3, gw3)
             ready = [jb for jb in made if (jb[1], units[jb[0]][1] // 4) in released]
             quota = min(S2_MAX, max(0, len(ready) - 4))
             if r >= NR - 4:
                 quota = 8
             taken = []
+            heads = []
             while ready and len(taken) < quota:
                 seen = []
                 rest = []
                 for jb in ready:
+                    if jb[0] in heads:
+                        continue
                     if jb[0] in seen or len(taken) >= quota:
                         rest.append(jb)
                     else:
                         seen.append(jb[0])
                         taken.append(jb)
+                        if HEAD_ON_SCALAR and jb[0] not in ndone:
+                            heads.append(jb[0])
                         s2_add(jb[0], jb[1])
                         if ndone[jb[0]] == NB - len(DIRECT.get(jb[0], [])):
                             t2_wait.append(jb[0])

@@ -21,28 +21,22 @@ NK = 512
 MCH = 512
 FLOPS = 2 * NB * NT * NK * NC
 
-MANUAL = True
-Z_BUFS = 0
-GRP_BUFS = 8
 LEAD = 3
-MC1_COPY = "ss"
-XOUT_LAG = 1
-FIN1_LAG = 1
-G_BUFS = 26
-ACC_BUFS = 7
-TQ_BUFS = 6
+G_BUFS = 20
+D_BUFS = 14
 X_BUFS = 4
-H_BUFS = 8
-REL = [[6, 7, 8, 9, 10, 12, 14, 16], [17, 18, 19, 20, 21, 22, 23, 24]]
-XA_FIRST = 5
-PREP1 = [14, 15, 16, 17, 18, 19, 20, 21]
-T2_PER_STEP = 1
-T2_LAG = 2
-W2_STEP = 9
-S2_MAX = 6
-HEAD_ON_SCALAR = False
-DIRECT = {13: [7], 14: [6, 7], 15: [5, 6, 7]}
-S1_ON_VECTOR = [1]
+H_BUFS = 6
+GRP_BUFS = 6
+H0_COPY = "ss"
+H1_COPY = "ss"
+D_QUOTA = 6
+ACC_LAG = 2
+ACC_PER_STEP = 1
+NOPOOL = [14, 15]
+X0_BASE = 0
+X1_BASE = 13
+H1_BASE = 5
+W2_STEP = -2
 
 
 def tile_dynamicmemorybank_pb_t_kernel(tc, h, x, memory, w2, b2, out):
@@ -53,18 +47,17 @@ def tile_dynamicmemorybank_pb_t_kernel(tc, h, x, memory, w2, b2, out):
         xstage = ctx.enter_context(tc.tile_pool(name="xstage", bufs=X_BUFS))
         grpp = ctx.enter_context(tc.tile_pool(name="grp", bufs=GRP_BUFS))
         gp = ctx.enter_context(tc.tile_pool(name="g", bufs=G_BUFS))
-        accp = ctx.enter_context(tc.tile_pool(name="acc", bufs=ACC_BUFS))
-        tqp = ctx.enter_context(tc.tile_pool(name="tq", bufs=TQ_BUFS))
+        dp = ctx.enter_context(tc.tile_pool(name="d", bufs=D_BUFS))
         otp = ctx.enter_context(tc.tile_pool(name="ot", bufs=3))
-        zp = ctx.enter_context(tc.psum_pool(name="z", bufs=Z_BUFS)) if Z_BUFS > 0 else None
-        auxp = ctx.enter_context(tc.psum_pool(name="aux", bufs=8 - Z_BUFS))
-        if MANUAL:
-            ctx.enter_context(tc.manual_schedule())
+        auxp = ctx.enter_context(tc.psum_pool(name="aux", bufs=8))
+        ctx.enter_context(tc.manual_schedule())
 
         ident = const.tile([P, P], F32, name="ident")
         make_identity(nc, ident[:])
+        identb = const.tile([P, P], BF16, name="identb")
+        make_identity(nc, identb[:])
         ones = const.tile([P, 2], BF16, name="ones")
-        nc.vector.memset(ones[:], 1.0 / 8192.0)
+        nc.vector.memset(ones[:], 1.0 / 1024.0)
         warm = const.tile([P, 1], F32, name="warm")
         nc.vector.memset(warm[:], 0.0)
         nc.scalar.activation(out=warm[:], in_=warm[:], func=ACT.Sigmoid)
@@ -92,13 +85,15 @@ def tile_dynamicmemorybank_pb_t_kernel(tc, h, x, memory, w2, b2, out):
             )
             hs[(b, mc)] = t
 
-        def load_mem(mc):
-            t = const.tile([P, 4096], BF16, name="mem%d" % mc)
+        def load_mem(mc, ch):
+            t = const.tile([P, 2048], BF16, name="mem%d_%d" % (mc, ch))
             nc.sync.dma_start(
-                out=t[:],
-                in_=memory[0, mc * MCH : (mc + 1) * MCH, :].rearrange("(p t) c -> p (t c)", t=4),
+                out=t[:].rearrange("p (t c) -> p t c", t=4),
+                in_=memory[0, mc * MCH : (mc + 1) * MCH, ch * 512 : (ch + 1) * 512].rearrange(
+                    "(p t) c -> p t c", t=4
+                ),
             )
-            mem[mc] = t
+            mem[(mc, ch)] = t
 
         def load_x(b, ch):
             t = xstage.tile([P, 4096], BF16, tag="xs", name="xs")
@@ -108,13 +103,15 @@ def tile_dynamicmemorybank_pb_t_kernel(tc, h, x, memory, w2, b2, out):
                 nc.sync.dma_start(out=tv[:, 4 * i : 4 * i + 4, :], in_=xv[:, 4 * i : 4 * i + 4, :])
             xs[(b, ch)] = t
 
-        loadq = [("h", b, 0) for b in range(NB)] + [("m", 0, 0)]
-        loadq += [("x", b, 0) for b in range(XA_FIRST)]
-        for i in range(4):
-            loadq += [("h", 2 * i, 1), ("h", 2 * i + 1, 1)]
-            if XA_FIRST + i < NB:
-                loadq += [("x", XA_FIRST + i, 0)]
-        loadq += [("m", 1, 0)] + [("x", b, 1) for b in range(NB)]
+        loadq = [("h", b, 0) for b in range(LEAD + 1)] + [("m", 0, 0)]
+        for b in range(NB):
+            loadq += [("x", b, 0)]
+            if b + LEAD + 1 < NB:
+                loadq += [("h", b + LEAD + 1, 0)]
+            else:
+                loadq += [("h", b + LEAD + 1 - NB, 1)]
+        loadq += [("h", b, 1) for b in range(LEAD + 1, NB)]
+        loadq += [("m", 1, 0), ("m", 0, 1)] + [("x", b, 1) for b in range(NB)] + [("m", 1, 1)]
         st = {"next": 0, "x": 1, "h": 0}
 
         def pump():
@@ -131,7 +128,7 @@ def tile_dynamicmemorybank_pb_t_kernel(tc, h, x, memory, w2, b2, out):
                     load_h(a0, a1)
                     st["h"] += 1
                 else:
-                    load_mem(a0)
+                    load_mem(a0, a1)
                 st["next"] += 1
 
         pump()
@@ -202,21 +199,16 @@ def tile_dynamicmemorybank_pb_t_kernel(tc, h, x, memory, w2, b2, out):
         units = [(mc, ct) for ch in range(2) for mc in range(2) for ct in range(4 * ch, 4 * ch + 4)]
         NU = len(units)
         gt = {}
-        s1 = {}
-        accs = {}
-        ndone = {}
-        tqs = {}
         U = {}
+        mT = {}
+        Dt = {}
+        ndone = {}
 
         def mx_sig(tiles):
             zs = []
-            for i, jb in enumerate(tiles):
-                j, b = jb
+            for j, b in tiles:
                 mc, ct = units[j]
-                if i < Z_BUFS:
-                    z = zp.tile([P, 512], F32, tag="z", name="z")
-                else:
-                    z = auxp.tile([P, 512], F32, tag="aux", name="z")
+                z = auxp.tile([P, 512], F32, tag="aux", name="z")
                 nc.tensor.matmul_mx(
                     out=z[:],
                     lhsT=w2c[ct // 4][:, (ct % 4) * P : (ct % 4 + 1) * P].bitcast(FP8X4),
@@ -235,109 +227,68 @@ def tile_dynamicmemorybank_pb_t_kernel(tc, h, x, memory, w2, b2, out):
                 )
                 gt[jb] = g
 
-        a1 = {}
-
-        def s1_vec(j, b):
-            g = gt[(j, b)]
-            if b == 0:
-                return
-            if b == 1:
-                a1[j] = accp.tile([P, 512], F32, tag="acc", name="a1")
-                nc.vector.tensor_tensor(out=a1[j][:], in0=gt[(j, 0)][:], in1=g[:], op=ALU.add)
-            else:
-                nc.vector.tensor_tensor(out=a1[j][:], in0=a1[j][:], in1=g[:], op=ALU.add)
-
-        def s1_vec_pe(j):
-            s1[j] = auxp.tile([P, 512], F32, tag="aux", name="s1")
-            for tt in range(4):
-                nc.tensor.transpose(
-                    s1[j][:, tt * P : (tt + 1) * P], a1[j][:, tt * P : (tt + 1) * P], ident[:]
-                )
-
-        def s1_add(tiles):
-            for j, b in tiles:
-                if j in S1_ON_VECTOR:
-                    continue
-                if b == 0:
-                    s1[j] = auxp.tile([P, 512], F32, tag="aux", name="s1")
-                g = gt[(j, b)]
+        def memT_pe(k):
+            t = auxp.tile([P, 1024], BF16, tag="aux", name="mT")
+            for u in range(2):
+                mc, ct = units[2 * k + u]
                 for tt in range(4):
-                    nc.tensor.matmul(
-                        out=s1[j][:, tt * P : (tt + 1) * P],
-                        lhsT=g[:, tt * P : (tt + 1) * P],
-                        rhs=ident[:],
-                        is_transpose=True,
-                        start=(b == 0 and tt == 0),
-                        stop=(b == NB - 1 and tt == 3),
+                    nc.tensor.transpose(
+                        t[:, u * 512 + tt * P : u * 512 + (tt + 1) * P],
+                        mem[(mc, ct // 4)][:, tt * 512 + (ct % 4) * P : tt * 512 + (ct % 4 + 1) * P],
+                        identb[:],
                     )
+            mT[k] = t
 
-        def s2_add(j, b):
+        def d_op(j, b):
             mc, ct = units[j]
-            g = gt[(j, b)]
             n = ndone.get(j, 0)
-            sc = U[(b, ct // 4)][:, ct % 4 : ct % 4 + 1]
-            if n == 0:
-                a = accp.tile([P, 512], F32, tag="acc", name="acc")
-                accs[j] = a
-                if HEAD_ON_SCALAR:
-                    nc.scalar.activation(out=a[:], in_=g[:], func=ACT.Copy, scale=sc)
-                else:
-                    nc.vector.tensor_scalar(out=a[:], in0=g[:], scalar1=sc, scalar2=None, op0=ALU.mult)
-            else:
-                a = accs[j]
-                nc.vector.scalar_tensor_tensor(
-                    out=a[:], in0=g[:], scalar=sc, in1=a[:], op0=ALU.mult, op1=ALU.add
-                )
-            ndone[j] = n + 1
-
-        def fin1(j):
-            mc, ct = units[j]
-            tq = tqp.tile([P, 512], F32, tag="tq", name="tq")
+            if n % 2 == 0:
+                Dt[(j, n // 2)] = dp.tile([P, 1024], F32, tag="d", name="d")
             nc.vector.scalar_tensor_tensor(
-                out=tq[:].rearrange("p (t c) -> p t c", t=4),
-                in0=s1[j][:].rearrange("p (t c) -> p t c", t=4),
-                scalar=8.0,
-                in1=mem[mc][:].rearrange("p (t c) -> p t c", t=4)[:, :, ct * P : (ct + 1) * P],
+                out=Dt[(j, n // 2)][:, (n % 2) * 512 : (n % 2 + 1) * 512],
+                in0=mT[j // 2][:, (j % 2) * 512 : (j % 2 + 1) * 512],
+                scalar=U[(b, ct // 4)][:, ct % 4 : ct % 4 + 1],
+                in1=gt[(j, b)][:],
                 op0=ALU.subtract,
                 op1=ALU.mult,
             )
-            tqs[j] = tq
-
-        t2s = {}
-        sgs = {}
-
-        def direct_scale(j, b):
-            ct = units[j][1]
-            sg = gp.tile([P, 512], F32, tag="g", name="sg")
-            nc.scalar.activation(
-                out=sg[:], in_=gt[(j, b)][:], func=ACT.Copy, scale=U[(b, ct // 4)][:, ct % 4 : ct % 4 + 1]
-            )
-            sgs[(j, b)] = sg
-
-        def t2_part(j, src, first, last):
-            if first:
-                t2s[j] = auxp.tile([P, 512], F32, tag="aux", name="t2")
-            for tt in range(4):
-                nc.tensor.matmul(
-                    out=t2s[j][:, tt * P : (tt + 1) * P],
-                    lhsT=src[:, tt * P : (tt + 1) * P],
-                    rhs=ident[:],
-                    is_transpose=True,
-                    start=(first and tt == 0),
-                    stop=(last and tt == 3),
+            ndone[j] = n + 1
+            if j not in NOPOOL and (n + 1) % 4 == 0:
+                q = (n + 1) // 4 - 1
+                nc.gpsimd.tensor_tensor(
+                    out=Dt[(j, 2 * q)][:], in0=Dt[(j, 2 * q)][:], in1=Dt[(j, 2 * q + 1)][:], op=ALU.add
                 )
 
-        def t2_pe(j):
-            ds = DIRECT.get(j, [])
-            for i, b in enumerate(ds):
-                t2_part(j, sgs[(j, b)], i == 0, False)
-            t2_part(j, accs[j], len(ds) == 0, True)
+        accs = {}
 
-        def fin2(j):
+        def acc_pe(j):
+            a = auxp.tile([P, 512], F32, tag="aux", name="acc")
+            srcs = [Dt[(j, i)] for i in (range(4) if j in NOPOOL else (0, 2))]
+            for i, s in enumerate(srcs):
+                for half in range(2):
+                    for tt in range(4):
+                        nc.tensor.matmul(
+                            out=a[:, tt * P : (tt + 1) * P],
+                            lhsT=s[:, half * 512 + tt * P : half * 512 + (tt + 1) * P],
+                            rhs=ident[:],
+                            is_transpose=True,
+                            start=(i == 0 and half == 0 and tt == 0),
+                            stop=(i == len(srcs) - 1 and half == 1 and tt == 3),
+                        )
+            accs[j] = a
+
+        def fin(j):
             mc, ct = units[j]
             ot = otp.tile([P, 512], F32, tag="ot", name="ot")
             nc.vector.scalar_tensor_tensor(
-                out=ot[:], in0=tqs[j][:], scalar=-0.125, in1=t2s[j][:], op0=ALU.mult, op1=ALU.add
+                out=ot[:].rearrange("p (t c) -> p t c", t=4),
+                in0=accs[j][:].rearrange("p (t c) -> p t c", t=4),
+                scalar=-0.125,
+                in1=mem[(mc, ct // 4)][:].rearrange("p (t c) -> p t c", t=4)[
+                    :, :, (ct % 4) * P : (ct % 4 + 1) * P
+                ],
+                op0=ALU.mult,
+                op1=ALU.add,
             )
             nc.sync.dma_start(
                 out=out[0, mc * MCH : (mc + 1) * MCH, ct * P : (ct + 1) * P].rearrange(
@@ -380,71 +331,60 @@ def tile_dynamicmemorybank_pb_t_kernel(tc, h, x, memory, w2, b2, out):
         nc.vector.tensor_copy(out=b2T[:], in_=b2ps[:, 0:8])
         w2_quant(1, gw1)
 
-        rounds = []
-        prep_at = {}
-        for j in range(0, NU, 2):
-            if j in (0, 4):
-                for b in range(NB):
-                    prep_at[len(rounds) + b - LEAD] = (b, j // 4)
-                rounds += [[(j, b), (j + 1, b)] for b in range(NB)]
-            else:
-                for jj in (j, j + 1):
-                    rounds.append([(jj, b) for b in range(4)])
-                    rounds.append([(jj, b) for b in range(4, 8)])
+        rounds = [[(j, b) for j in range(4)] for b in range(NB)]
+        first_round = {0: 0, 1: 0}
+        for k in range(2, NU // 2):
+            first_round[k] = len(rounds)
+            for bb in range(0, NB, 2):
+                rounds.append([(2 * k, bb), (2 * k + 1, bb), (2 * k, bb + 1), (2 * k + 1, bb + 1)])
         NR = len(rounds)
-        t2_wait = []
-        t2_age = {}
-        fin2_wait = []
-        fin1_wait = []
-        xout_wait = []
+        prep_at = {}
+        for b in range(NB):
+            prep_at.setdefault(b - LEAD, []).append((b, 0))
+            prep_at.setdefault(H1_BASE + b // 2, []).append((b, 1))
+        xrel = {}
+        for b in range(NB):
+            xrel.setdefault(b + X0_BASE, []).append((b, 0))
+            xrel.setdefault(X1_BASE + (3 * b) // 4, []).append((b, 1))
+
         made = []
         released = []
-        s1v_pe = []
+        acc_wait = []
+        fin_wait = []
+        xout_wait = []
         copy_wait = []
         quant_wait = []
 
-        for r in range(-LEAD, NR + 8):
+        for r in range(-LEAD, NR + 12):
             if 0 <= r < NR:
                 mx_sig(rounds[r])
-            for ch in range(2):
-                for b in range(NB):
-                    if REL[ch][b] == r:
-                        xmean_pe(b, ch)
-                        xout_wait.append((r, b, ch))
-            if 1 <= r <= NR:
-                s1_add(rounds[r - 1])
-                for j, b in rounds[r - 1]:
-                    if b == NB - 1 and j not in S1_ON_VECTOR:
-                        fin1_wait.append((r, j))
-            for j in s1v_pe:
-                s1_vec_pe(j)
-                fin1_wait.append((r, j))
-            s1v_pe = []
-            now_t2 = [j for j in t2_wait if t2_age[j] + T2_LAG <= r][:T2_PER_STEP]
-            t2_wait = [j for j in t2_wait if j not in now_t2]
-            for j in now_t2:
-                t2_pe(j)
+            new_xout = []
+            for b, ch in xrel.get(r, []):
+                xmean_pe(b, ch)
+                new_xout.append((b, ch))
+            now_acc = [j for rr, j in acc_wait if rr + (1 if j in NOPOOL else ACC_LAG) <= r][:ACC_PER_STEP]
+            acc_wait = [e for e in acc_wait if e[1] not in now_acc]
+            for j in now_acc:
+                acc_pe(j)
+            for k in range(NU // 2):
+                if first_round[k] == r:
+                    memT_pe(k)
             new_copy = []
-            if r in prep_at:
-                new_copy.append(prep_pe(prep_at[r][0], prep_at[r][1]))
+            for b, mc in prep_at.get(r, []):
+                new_copy.append(prep_pe(b, mc))
             new_quant = []
             for job in copy_wait:
-                engs = "vs" if job[1] == 0 else MC1_COPY
+                engs = H0_COPY if job[1] == 0 else H1_COPY
                 new_quant.append(prep_copy(job, 0, engs[0]))
                 new_quant.append(prep_copy(job, 1, engs[1]))
             copy_wait = new_copy
-            for rr, j in fin1_wait:
-                if rr + FIN1_LAG <= r:
-                    fin1(j)
-            fin1_wait = [e for e in fin1_wait if e[0] + FIN1_LAG > r]
-            for rr, b, ch in xout_wait:
-                if rr + XOUT_LAG <= r:
-                    xmean_out(b, ch)
-                    released.append((b, ch))
-            xout_wait = [e for e in xout_wait if e[0] + XOUT_LAG > r]
-            for j in fin2_wait:
-                fin2(j)
-            fin2_wait = now_t2
+            for b, ch in xout_wait:
+                xmean_out(b, ch)
+                released.append((b, ch))
+            xout_wait = new_xout
+            for j in fin_wait:
+                fin(j)
+            fin_wait = now_acc
             prep_h_back(quant_wait)
             quant_wait = new_quant
             if r == W2_STEP:
@@ -456,37 +396,14 @@ def tile_dynamicmemorybank_pb_t_kernel(tc, h, x, memory, w2, b2, out):
                 w2_quant(2, gw2)
                 w2_quant(3, gw3)
             if 1 <= r <= NR:
-                for j, b in rounds[r - 1]:
-                    if j in S1_ON_VECTOR:
-                        s1_vec(j, b)
-                        if b == NB - 1:
-                            s1v_pe.append(j)
-                    if b in DIRECT.get(j, []):
-                        direct_scale(j, b)
-                    else:
-                        made.append((j, b))
-            ready = [jb for jb in made if (jb[1], units[jb[0]][1] // 4) in released]
-            quota = min(S2_MAX, max(0, len(ready) - 4))
-            if r >= NR - 4:
-                quota = 8
-            taken = []
-            heads = []
-            while ready and len(taken) < quota:
-                seen = []
-                rest = []
-                for jb in ready:
-                    if jb[0] in heads:
-                        continue
-                    if jb[0] in seen or len(taken) >= quota:
-                        rest.append(jb)
-                    else:
-                        seen.append(jb[0])
-                        taken.append(jb)
-                        if HEAD_ON_SCALAR and jb[0] not in ndone:
-                            heads.append(jb[0])
-                        s2_add(jb[0], jb[1])
-                        if ndone[jb[0]] == NB - len(DIRECT.get(jb[0], [])):
-                            t2_wait.append(jb[0])
-                            t2_age[jb[0]] = r
-                ready = rest
-            made = [jb for jb in made if jb not in taken]
+                made += rounds[r - 1]
+            taken = 0
+            while made and taken < D_QUOTA:
+                j, b = made[0]
+                if (b, units[j][1] // 4) not in released:
+                    break
+                made = made[1:]
+                d_op(j, b)
+                taken += 1
+                if ndone[j] == NB:
+                    acc_wait.append((r, j))

@@ -36,7 +36,17 @@ NOPOOL = [14, 15]
 X0_BASE = 0
 X1_BASE = 13
 H1_BASE = 5
-W2_STEP = -2
+W2_STEP = 13
+PH2_G4 = True
+H1_EARLY = 2
+MT_LEAD = 0
+GAP = 1
+MANUAL = True
+W2_ENG = "g"
+POOL_SPLIT = 1
+M1_POS = 1
+STORE_LAG = 2
+OT_BUFS = 5
 
 
 def tile_dynamicmemorybank_pb_t_kernel(tc, h, x, memory, w2, b2, out):
@@ -48,9 +58,10 @@ def tile_dynamicmemorybank_pb_t_kernel(tc, h, x, memory, w2, b2, out):
         grpp = ctx.enter_context(tc.tile_pool(name="grp", bufs=GRP_BUFS))
         gp = ctx.enter_context(tc.tile_pool(name="g", bufs=G_BUFS))
         dp = ctx.enter_context(tc.tile_pool(name="d", bufs=D_BUFS))
-        otp = ctx.enter_context(tc.tile_pool(name="ot", bufs=3))
+        otp = ctx.enter_context(tc.tile_pool(name="ot", bufs=OT_BUFS))
         auxp = ctx.enter_context(tc.psum_pool(name="aux", bufs=8))
-        ctx.enter_context(tc.manual_schedule())
+        if MANUAL:
+            ctx.enter_context(tc.manual_schedule())
 
         ident = const.tile([P, P], F32, name="ident")
         make_identity(nc, ident[:])
@@ -64,14 +75,20 @@ def tile_dynamicmemorybank_pb_t_kernel(tc, h, x, memory, w2, b2, out):
         bzf = const.tile([P, P], F32, name="bzf")
         nc.vector.memset(bzf[:], 0.0)
 
-        w2raw = xstage.tile([P, 4096], BF16, tag="xs", name="w2raw")
-        for u in range(2):
-            nc.sync.dma_start(
-                out=w2raw[:, u * 2048 : (u + 1) * 2048],
-                in_=w2[u * 256 : (u + 1) * 256, :].rearrange("(q e) c -> q (e c)", e=2),
-            )
+        w2raw = {}
+
+        def load_w2(ch):
+            t = hstage.tile([P, 2048], BF16, tag="hs", name="w2raw")
+            for u in range(2):
+                nc.sync.dma_start(
+                    out=t[:, u * 1024 : (u + 1) * 1024].rearrange("p (e c) -> p e c", e=2),
+                    in_=w2[u * 256 : (u + 1) * 256, ch * 512 : (ch + 1) * 512].rearrange(
+                        "(q e) c -> q e c", e=2
+                    ),
+                )
+            w2raw[ch] = t
+
         b2r = const.tile([8, P], BF16, name="b2r")
-        nc.sync.dma_start(out=b2r[:], in_=b2.rearrange("(r c) -> r c", c=P))
 
         hs = {}
         xs = {}
@@ -103,23 +120,24 @@ def tile_dynamicmemorybank_pb_t_kernel(tc, h, x, memory, w2, b2, out):
                 nc.sync.dma_start(out=tv[:, 4 * i : 4 * i + 4, :], in_=xv[:, 4 * i : 4 * i + 4, :])
             xs[(b, ch)] = t
 
-        loadq = [("h", b, 0) for b in range(LEAD + 1)] + [("m", 0, 0)]
+        loadq = [("h", 0, 0), ("w", 0, 0), ("b", 0, 0)] + [("h", b, 0) for b in range(1, LEAD + 1)] + [("m", 0, 0)]
         for b in range(NB):
             loadq += [("x", b, 0)]
             if b + LEAD + 1 < NB:
                 loadq += [("h", b + LEAD + 1, 0)]
-            else:
+            elif b + LEAD + 1 - NB < H1_EARLY:
                 loadq += [("h", b + LEAD + 1 - NB, 1)]
-        loadq += [("h", b, 1) for b in range(LEAD + 1, NB)]
-        loadq += [("m", 1, 0), ("m", 0, 1)] + [("x", b, 1) for b in range(NB)] + [("m", 1, 1)]
-        st = {"next": 0, "x": 1, "h": 0}
+        h1rest = [("h", b, 1) for b in range(min(H1_EARLY, LEAD + 1), NB)]
+        loadq += h1rest[:M1_POS] + [("m", 1, 0)] + h1rest[M1_POS:]
+        loadq += [("w", 1, 0), ("m", 0, 1)] + [("x", b, 1) for b in range(NB)] + [("m", 1, 1)]
+        st = {"next": 0, "x": 0, "h": 0}
 
         def pump():
             while st["next"] < len(loadq):
                 kind, a0, a1 = loadq[st["next"]]
                 if kind == "x" and st["x"] >= X_BUFS:
                     return
-                if kind == "h" and st["h"] >= H_BUFS:
+                if kind in ("h", "w") and st["h"] >= H_BUFS:
                     return
                 if kind == "x":
                     load_x(a0, a1)
@@ -127,6 +145,11 @@ def tile_dynamicmemorybank_pb_t_kernel(tc, h, x, memory, w2, b2, out):
                 elif kind == "h":
                     load_h(a0, a1)
                     st["h"] += 1
+                elif kind == "w":
+                    load_w2(a0)
+                    st["h"] += 1
+                elif kind == "b":
+                    nc.sync.dma_start(out=b2r[:], in_=b2.rearrange("(r c) -> r c", c=P))
                 else:
                     load_mem(a0, a1)
                 st["next"] += 1
@@ -135,14 +158,15 @@ def tile_dynamicmemorybank_pb_t_kernel(tc, h, x, memory, w2, b2, out):
 
         w2c = [const.tile([P, 512], U32, name="w2c%d" % i, align_bytes=64) for i in range(2)]
         w2s = [const.tile([P, 512], U8, name="w2s%d" % i, align_bytes=64) for i in range(2)]
-        w2v = w2raw[:].rearrange("p (t c) -> p c t", t=4)
 
         def w2_regroup(q, eng):
             gw = grpp.tile([P, 1024], BF16, tag="grp", name="gw", align_bytes=64)
             dst = gw[:].rearrange("p (c t) -> p c t", t=4)
-            src = w2v[:, q * 256 : (q + 1) * 256, :]
+            src = w2raw[q // 2][:].rearrange("p (t c) -> p c t", t=4)[:, (q % 2) * 256 : (q % 2 + 1) * 256, :]
             if eng == "v":
                 nc.vector.tensor_copy(out=dst, in_=src)
+            elif eng == "g":
+                nc.gpsimd.tensor_scalar(out=dst, in0=src, scalar1=1.0, scalar2=0.0, op0=ALU.mult, op1=ALU.add)
             else:
                 nc.scalar.copy(out=dst, in_=src)
             return gw
@@ -255,16 +279,25 @@ def tile_dynamicmemorybank_pb_t_kernel(tc, h, x, memory, w2, b2, out):
             ndone[j] = n + 1
             if j not in NOPOOL and (n + 1) % 4 == 0:
                 q = (n + 1) // 4 - 1
-                nc.gpsimd.tensor_tensor(
-                    out=Dt[(j, 2 * q)][:], in0=Dt[(j, 2 * q)][:], in1=Dt[(j, 2 * q + 1)][:], op=ALU.add
-                )
+                for s in range(POOL_SPLIT):
+                    wd = 1024 // POOL_SPLIT
+                    nc.gpsimd.tensor_tensor(
+                        out=Dt[(j, 2 * q)][:, s * wd : (s + 1) * wd],
+                        in0=Dt[(j, 2 * q)][:, s * wd : (s + 1) * wd],
+                        in1=Dt[(j, 2 * q + 1)][:, s * wd : (s + 1) * wd],
+                        op=ALU.add,
+                    )
 
         accs = {}
+        ots = {}
 
-        def acc_pe(j):
-            a = auxp.tile([P, 512], F32, tag="aux", name="acc")
-            srcs = [Dt[(j, i)] for i in (range(4) if j in NOPOOL else (0, 2))]
-            for i, s in enumerate(srcs):
+        def acc_pe(j, parts):
+            if parts[0] == 0:
+                accs[j] = auxp.tile([P, 512], F32, tag="aux", name="acc")
+            a = accs[j]
+            lastp = 3 if j in NOPOOL else 2
+            for i in parts:
+                s = Dt[(j, i)]
                 for half in range(2):
                     for tt in range(4):
                         nc.tensor.matmul(
@@ -273,9 +306,8 @@ def tile_dynamicmemorybank_pb_t_kernel(tc, h, x, memory, w2, b2, out):
                             rhs=ident[:],
                             is_transpose=True,
                             start=(i == 0 and half == 0 and tt == 0),
-                            stop=(i == len(srcs) - 1 and half == 1 and tt == 3),
+                            stop=(i == lastp and half == 1 and tt == 3),
                         )
-            accs[j] = a
 
         def fin(j):
             mc, ct = units[j]
@@ -290,11 +322,15 @@ def tile_dynamicmemorybank_pb_t_kernel(tc, h, x, memory, w2, b2, out):
                 op0=ALU.mult,
                 op1=ALU.add,
             )
+            ots[j] = ot
+
+        def store(j):
+            mc, ct = units[j]
             nc.sync.dma_start(
                 out=out[0, mc * MCH : (mc + 1) * MCH, ct * P : (ct + 1) * P].rearrange(
                     "(p t) c -> p t c", t=4
                 ),
-                in_=ot[:].rearrange("p (t c) -> p t c", t=4),
+                in_=ots[j][:].rearrange("p (t c) -> p t c", t=4),
             )
 
         xps = {}
@@ -323,6 +359,8 @@ def tile_dynamicmemorybank_pb_t_kernel(tc, h, x, memory, w2, b2, out):
 
         gw0 = w2_regroup(0, "v")
         gw1 = w2_regroup(1, "s")
+        st["h"] -= 1
+        pump()
         nc.vector.tensor_copy(out=bzf[0:8, :], in_=b2r[:])
         b2ps = auxp.tile([P, 512], F32, tag="aux", name="b2ps")
         nc.tensor.transpose(b2ps[:, 0:P], bzf[:], ident[:])
@@ -333,22 +371,39 @@ def tile_dynamicmemorybank_pb_t_kernel(tc, h, x, memory, w2, b2, out):
 
         rounds = [[(j, b) for j in range(4)] for b in range(NB)]
         first_round = {0: 0, 1: 0}
-        for k in range(2, NU // 2):
+        k0 = 2
+        if PH2_G4:
+            rounds += [[] for i in range(GAP)]
+            first_round[2] = NB + GAP
+            first_round[3] = NB + GAP
+            rounds += [[(j, b) for j in range(4, 8)] for b in range(NB)]
+            k0 = 4
+        for k in range(k0, NU // 2):
             first_round[k] = len(rounds)
-            for bb in range(0, NB, 2):
-                rounds.append([(2 * k, bb), (2 * k + 1, bb), (2 * k, bb + 1), (2 * k + 1, bb + 1)])
+            if k == NU // 2 - 1:
+                for j in (2 * k, 2 * k + 1):
+                    rounds.append([(j, b) for b in range(4)])
+                    rounds.append([(j, b) for b in range(4, 8)])
+            else:
+                for bb in range(0, NB, 2):
+                    rounds.append([(2 * k, bb), (2 * k + 1, bb), (2 * k, bb + 1), (2 * k + 1, bb + 1)])
         NR = len(rounds)
         prep_at = {}
         for b in range(NB):
             prep_at.setdefault(b - LEAD, []).append((b, 0))
-            prep_at.setdefault(H1_BASE + b // 2, []).append((b, 1))
+            if PH2_G4:
+                prep_at.setdefault(NB + GAP + b - LEAD, []).append((b, 1))
+            else:
+                prep_at.setdefault(H1_BASE + b // 2, []).append((b, 1))
         xrel = {}
         for b in range(NB):
             xrel.setdefault(b + X0_BASE, []).append((b, 0))
-            xrel.setdefault(X1_BASE + (3 * b) // 4, []).append((b, 1))
+            xrel.setdefault(X1_BASE + GAP + (3 * b) // 4, []).append((b, 1))
 
         made = []
         released = []
+        store_wait = []
+        part_wait = []
         acc_wait = []
         fin_wait = []
         xout_wait = []
@@ -356,41 +411,52 @@ def tile_dynamicmemorybank_pb_t_kernel(tc, h, x, memory, w2, b2, out):
         quant_wait = []
 
         for r in range(-LEAD, NR + 12):
-            if 0 <= r < NR:
-                mx_sig(rounds[r])
-            new_xout = []
-            for b, ch in xrel.get(r, []):
-                xmean_pe(b, ch)
-                new_xout.append((b, ch))
-            now_acc = [j for rr, j in acc_wait if rr + (1 if j in NOPOOL else ACC_LAG) <= r][:ACC_PER_STEP]
-            acc_wait = [e for e in acc_wait if e[1] not in now_acc]
-            for j in now_acc:
-                acc_pe(j)
-            for k in range(NU // 2):
-                if first_round[k] == r:
-                    memT_pe(k)
-            new_copy = []
-            for b, mc in prep_at.get(r, []):
-                new_copy.append(prep_pe(b, mc))
             new_quant = []
             for job in copy_wait:
                 engs = H0_COPY if job[1] == 0 else H1_COPY
                 new_quant.append(prep_copy(job, 0, engs[0]))
                 new_quant.append(prep_copy(job, 1, engs[1]))
+            if 0 <= r < NR:
+                mx_sig(rounds[r])
+            new_copy = []
+            for b, mc in prep_at.get(r, []):
+                new_copy.append(prep_pe(b, mc))
+            new_xout = []
+            for b, ch in xrel.get(r, []):
+                xmean_pe(b, ch)
+                new_xout.append((b, ch))
+            now_acc = [j for rr, j in acc_wait if rr + ACC_LAG <= r][:ACC_PER_STEP]
+            acc_wait = [e for e in acc_wait if e[1] not in now_acc]
+            for j in now_acc:
+                acc_pe(j, [0, 2])
+            for j, i in part_wait:
+                acc_pe(j, [i])
+                if i == 3:
+                    now_acc.append(j)
+            part_wait = []
+            for k in range(NU // 2):
+                if first_round[k] - MT_LEAD == r:
+                    memT_pe(k)
             copy_wait = new_copy
             for b, ch in xout_wait:
                 xmean_out(b, ch)
                 released.append((b, ch))
             xout_wait = new_xout
+            for rr, j in store_wait:
+                if rr + (STORE_LAG if r < NR else 0) <= r:
+                    store(j)
+            store_wait = [e for e in store_wait if e[0] + (STORE_LAG if r < NR else 0) > r]
             for j in fin_wait:
                 fin(j)
+                if r >= NR:
+                    store(j)
+                else:
+                    store_wait.append((r, j))
             fin_wait = now_acc
-            prep_h_back(quant_wait)
-            quant_wait = new_quant
             if r == W2_STEP:
-                gw2 = w2_regroup(2, "s")
-                gw3 = w2_regroup(3, "s")
-                st["x"] -= 1
+                gw2 = w2_regroup(2, W2_ENG)
+                gw3 = w2_regroup(3, W2_ENG)
+                st["h"] -= 1
                 pump()
             if r == W2_STEP + 1:
                 w2_quant(2, gw2)
@@ -405,5 +471,9 @@ def tile_dynamicmemorybank_pb_t_kernel(tc, h, x, memory, w2, b2, out):
                 made = made[1:]
                 d_op(j, b)
                 taken += 1
-                if ndone[j] == NB:
+                if j in NOPOOL:
+                    if ndone[j] % 2 == 0:
+                        part_wait.append((j, ndone[j] // 2 - 1))
+                elif ndone[j] == NB:
                     acc_wait.append((r, j))
+            prep_h_back(new_quant)

@@ -22,21 +22,22 @@ MCH = 512
 FLOPS = 2 * NB * NT * NK * NC
 
 LEAD = 3
-G_BUFS = 20
+G_BUFS = 10
 D_BUFS = 14
 X_BUFS = 4
 H_BUFS = 6
 GRP_BUFS = 6
-H0_COPY = "ss"
-H1_COPY = "ss"
+H0_COPY = ["ss", "ss"]
+H1_COPY = ["ss", "ss"]
 D_QUOTA = 6
 ACC_LAG = 2
+ACC_LAG_W = 3
 ACC_PER_STEP = 1
 NOPOOL = [14, 15]
 X0_BASE = 0
 X1_BASE = 13
 H1_BASE = 5
-W2_STEP = 13
+W2_STEP = 12
 PH2_G4 = True
 H1_EARLY = 2
 MT_LEAD = 0
@@ -129,7 +130,7 @@ def tile_dynamicmemorybank_pb_t_kernel(tc, h, x, memory, w2, b2, out):
                 loadq += [("h", b + LEAD + 1 - NB, 1)]
         h1rest = [("h", b, 1) for b in range(min(H1_EARLY, LEAD + 1), NB)]
         loadq += h1rest[:M1_POS] + [("m", 1, 0)] + h1rest[M1_POS:]
-        loadq += [("w", 1, 0), ("m", 0, 1)] + [("x", b, 1) for b in range(NB)] + [("m", 1, 1)]
+        loadq += [("w", 1, 0), ("m", 0, 1), ("m", 1, 1)] + [("x", b, 1) for b in range(NB)]
         st = {"next": 0, "x": 0, "h": 0}
 
         def pump():
@@ -220,13 +221,19 @@ def tile_dynamicmemorybank_pb_t_kernel(tc, h, x, memory, w2, b2, out):
                     in_=gh[:],
                 )
 
-        units = [(mc, ct) for ch in range(2) for mc in range(2) for ct in range(4 * ch, 4 * ch + 4)]
+        units = [(mc, ct) for mc in range(2) for ct in range(4)] + [(mc, ct) for ct in range(4, 8) for mc in range(2)]
+        WIDE = [4, 5, 6]
         NU = len(units)
-        gt = {}
+        gg = {}
         U = {}
         mT = {}
         Dt = {}
         ndone = {}
+
+        def gkey(j, b):
+            if j in NOPOOL:
+                return ("n", j, b // 2), b % 2
+            return (j // 2, b), j % 2
 
         def mx_sig(tiles):
             zs = []
@@ -245,11 +252,16 @@ def tile_dynamicmemorybank_pb_t_kernel(tc, h, x, memory, w2, b2, out):
                 zs.append(z)
             for jb, z in zip(tiles, zs):
                 ct = units[jb[0]][1]
-                g = gp.tile([P, 512], F32, tag="g", name="g")
+                key, half = gkey(jb[0], jb[1])
+                if key not in gg:
+                    gg[key] = gp.tile([P, 1024], F32, tag="g", name="g")
                 nc.scalar.activation(
-                    out=g[:], in_=z[:], func=ACT.Sigmoid, bias=b2T[:, ct : ct + 1], scale=1.0
+                    out=gg[key][:, half * 512 : (half + 1) * 512],
+                    in_=z[:],
+                    func=ACT.Sigmoid,
+                    bias=b2T[:, ct : ct + 1],
+                    scale=1.0,
                 )
-                gt[jb] = g
 
         def memT_pe(k):
             t = auxp.tile([P, 1024], BF16, tag="aux", name="mT")
@@ -272,7 +284,7 @@ def tile_dynamicmemorybank_pb_t_kernel(tc, h, x, memory, w2, b2, out):
                 out=Dt[(j, n // 2)][:, (n % 2) * 512 : (n % 2 + 1) * 512],
                 in0=mT[j // 2][:, (j % 2) * 512 : (j % 2 + 1) * 512],
                 scalar=U[(b, ct // 4)][:, ct % 4 : ct % 4 + 1],
-                in1=gt[(j, b)][:],
+                in1=gg[gkey(j, b)[0]][:, gkey(j, b)[1] * 512 : (gkey(j, b)[1] + 1) * 512],
                 op0=ALU.subtract,
                 op1=ALU.mult,
             )
@@ -286,6 +298,37 @@ def tile_dynamicmemorybank_pb_t_kernel(tc, h, x, memory, w2, b2, out):
                         in0=Dt[(j, 2 * q)][:, s * wd : (s + 1) * wd],
                         in1=Dt[(j, 2 * q + 1)][:, s * wd : (s + 1) * wd],
                         op=ALU.add,
+                    )
+
+        def d_wide(k, b):
+            ct = units[2 * k][1]
+            n = ndone.get(("w", k), 0)
+            Dt[("w", k, n)] = dp.tile([P, 1024], F32, tag="d", name="d")
+            nc.vector.scalar_tensor_tensor(
+                out=Dt[("w", k, n)][:],
+                in0=mT[k][:],
+                scalar=U[(b, ct // 4)][:, ct % 4 : ct % 4 + 1],
+                in1=gg[(k, b)][:],
+                op0=ALU.subtract,
+                op1=ALU.mult,
+            )
+            ndone[("w", k)] = n + 1
+            if n % 2 == 1:
+                nc.gpsimd.tensor_tensor(
+                    out=Dt[("w", k, n - 1)][:], in0=Dt[("w", k, n - 1)][:], in1=Dt[("w", k, n)][:], op=ALU.add
+                )
+
+        def acc_wide(j):
+            accs[j] = auxp.tile([P, 512], F32, tag="aux", name="acc")
+            for q in range(4):
+                for tt in range(4):
+                    nc.tensor.matmul(
+                        out=accs[j][:, tt * P : (tt + 1) * P],
+                        lhsT=Dt[("w", j // 2, 2 * q)][:, (j % 2) * 512 + tt * P : (j % 2) * 512 + (tt + 1) * P],
+                        rhs=ident[:],
+                        is_transpose=True,
+                        start=(q == 0 and tt == 0),
+                        stop=(q == 3 and tt == 3),
                     )
 
         accs = {}
@@ -413,7 +456,7 @@ def tile_dynamicmemorybank_pb_t_kernel(tc, h, x, memory, w2, b2, out):
         for r in range(-LEAD, NR + 12):
             new_quant = []
             for job in copy_wait:
-                engs = H0_COPY if job[1] == 0 else H1_COPY
+                engs = (H0_COPY if job[1] == 0 else H1_COPY)[job[0] % 2]
                 new_quant.append(prep_copy(job, 0, engs[0]))
                 new_quant.append(prep_copy(job, 1, engs[1]))
             if 0 <= r < NR:
@@ -425,10 +468,13 @@ def tile_dynamicmemorybank_pb_t_kernel(tc, h, x, memory, w2, b2, out):
             for b, ch in xrel.get(r, []):
                 xmean_pe(b, ch)
                 new_xout.append((b, ch))
-            now_acc = [j for rr, j in acc_wait if rr + ACC_LAG <= r][:ACC_PER_STEP]
+            now_acc = [j for rr, j in acc_wait if rr + (ACC_LAG_W if j // 2 in WIDE else ACC_LAG) <= r][:ACC_PER_STEP]
             acc_wait = [e for e in acc_wait if e[1] not in now_acc]
             for j in now_acc:
-                acc_pe(j, [0, 2])
+                if j // 2 in WIDE:
+                    acc_wide(j)
+                else:
+                    acc_pe(j, [0, 2])
             for j, i in part_wait:
                 acc_pe(j, [i])
                 if i == 3:
@@ -462,13 +508,20 @@ def tile_dynamicmemorybank_pb_t_kernel(tc, h, x, memory, w2, b2, out):
                 w2_quant(2, gw2)
                 w2_quant(3, gw3)
             if 1 <= r <= NR:
-                made += rounds[r - 1]
+                made += [jb for jb in rounds[r - 1] if jb[0] // 2 not in WIDE or jb[0] % 2 == 1]
             taken = 0
             while made and taken < D_QUOTA:
                 j, b = made[0]
                 if (b, units[j][1] // 4) not in released:
                     break
                 made = made[1:]
+                if j // 2 in WIDE:
+                    d_wide(j // 2, b)
+                    taken += 2
+                    if ndone[("w", j // 2)] == NB:
+                        acc_wait.append((r, j - 1))
+                        acc_wait.append((r, j))
+                    continue
                 d_op(j, b)
                 taken += 1
                 if j in NOPOOL:

@@ -34,13 +34,14 @@ ACC_LAG = 2
 ACC_LAG_W = 3
 ACC_PER_STEP = 1
 NOPOOL = [14, 15]
-X0_BASE = 0
+X0_BASE = 1
 X1_BASE = 13
 H1_BASE = 5
 W2_STEP = 12
 PH2_G4 = True
 H1_EARLY = 2
 MT_LEAD = 0
+XFIRST = True
 GAP = 1
 MANUAL = True
 W2_ENG = "g"
@@ -462,12 +463,17 @@ def tile_dynamicmemorybank_pb_t_kernel(tc, h, x, memory, w2, b2, out):
             if 0 <= r < NR:
                 mx_sig(rounds[r])
             new_copy = []
+            new_xout = []
+            if XFIRST:
+                for b, ch in xrel.get(r, []):
+                    xmean_pe(b, ch)
+                    new_xout.append((b, ch))
             for b, mc in prep_at.get(r, []):
                 new_copy.append(prep_pe(b, mc))
-            new_xout = []
-            for b, ch in xrel.get(r, []):
-                xmean_pe(b, ch)
-                new_xout.append((b, ch))
+            if not XFIRST:
+                for b, ch in xrel.get(r, []):
+                    xmean_pe(b, ch)
+                    new_xout.append((b, ch))
             now_acc = [j for rr, j in acc_wait if rr + (ACC_LAG_W if j // 2 in WIDE else ACC_LAG) <= r][:ACC_PER_STEP]
             acc_wait = [e for e in acc_wait if e[1] not in now_acc]
             for j in now_acc:

@@ -47,7 +47,7 @@ MANUAL = True
 W2_ENG = "g"
 POOL_SPLIT = 1
 M1_POS = 1
-STORE_LAG = 2
+STORE_LAG = 4
 OT_BUFS = 5
 
 
@@ -442,7 +442,7 @@ def tile_dynamicmemorybank_pb_t_kernel(tc, h, x, memory, w2, b2, out):
         xrel = {}
         for b in range(NB):
             xrel.setdefault(b + X0_BASE, []).append((b, 0))
-            xrel.setdefault(X1_BASE + GAP + (3 * b) // 4, []).append((b, 1))
+            xrel.setdefault(X1_BASE + GAP + (6 * b) // 7, []).append((b, 1))
 
         made = []
         released = []

from contextlib import ExitStack

import concourse.bass as bass
import concourse.mybir as mybir
import concourse.tile as tile
from concourse.masks import make_identity

F32 = mybir.dt.float32
BF16 = mybir.dt.bfloat16
U32 = mybir.dt.uint32
U8 = mybir.dt.uint8
FP8X4 = mybir.dt.float8_e4m3fn_x4
ALU = mybir.AluOpType
ACT = mybir.ActivationFunctionType

P = 128
NB = 8
NT = 1024
NC = 1024
NK = 512
MCH = 512
FLOPS = 2 * NB * NT * NK * NC

LEAD = 3
G_BUFS = 10
D_BUFS = 14
X_BUFS = 4
H_BUFS = 6
GRP_BUFS = 6
H0_COPY = ["ss", "ss"]
H1_COPY = ["ss", "ss"]
D_QUOTA = 6
ACC_LAG = 2
ACC_LAG_W = 3
ACC_PER_STEP = 1
NOPOOL = [14, 15]
X0_BASE = 1
X1_BASE = 13
H1_BASE = 5
W2_STEP = 12
PH2_G4 = True
H1_EARLY = 2
MT_LEAD = 0
XFIRST = True
GAP = 1
MANUAL = True
W2_ENG = "g"
POOL_SPLIT = 1
M1_POS = 1
STORE_LAG = 4
OT_BUFS = 5


def tile_dynamicmemorybank_pb_t_kernel(tc, h, x, memory, w2, b2, out):
    nc = tc.nc
    with ExitStack() as ctx:
        const = ctx.enter_context(tc.tile_pool(name="const", bufs=1))
        hstage = ctx.enter_context(tc.tile_pool(name="hstage", bufs=H_BUFS))
        xstage = ctx.enter_context(tc.tile_pool(name="xstage", bufs=X_BUFS))
        grpp = ctx.enter_context(tc.tile_pool(name="grp", bufs=GRP_BUFS))
        gp = ctx.enter_context(tc.tile_pool(name="g", bufs=G_BUFS))
        dp = ctx.enter_context(tc.tile_pool(name="d", bufs=D_BUFS))
        otp = ctx.enter_context(tc.tile_pool(name="ot", bufs=OT_BUFS))
        auxp = ctx.enter_context(tc.psum_pool(name="aux", bufs=8))
        if MANUAL:
            ctx.enter_context(tc.manual_schedule())

        ident = const.tile([P, P], F32, name="ident")
        make_identity(nc, ident[:])
        identb = const.tile([P, P], BF16, name="identb")
        make_identity(nc, identb[:])
        ones = const.tile([P, 2], BF16, name="ones")
        nc.vector.memset(ones[:], 1.0 / 1024.0)
        warm = const.tile([P, 1], F32, name="warm")
        nc.vector.memset(warm[:], 0.0)
        nc.scalar.activation(out=warm[:], in_=warm[:], func=ACT.Sigmoid)
        bzf = const.tile([P, P], F32, name="bzf")
        nc.vector.memset(bzf[:], 0.0)

        w2raw = {}

        def load_w2(ch):
            t = hstage.tile([P, 2048], BF16, tag="hs", name="w2raw")
            for u in range(2):
                nc.sync.dma_start(
                    out=t[:, u * 1024 : (u + 1) * 1024].rearrange("p (e c) -> p e c", e=2),
                    in_=w2[u * 256 : (u + 1) * 256, ch * 512 : (ch + 1) * 512].rearrange(
                        "(q e) c -> q e c", e=2
                    ),
                )
            w2raw[ch] = t

        b2r = const.tile([8, P], BF16, name="b2r")

        hs = {}
        xs = {}
        mem = {}

        def load_h(b, mc):
            t = hstage.tile([P, 2048], BF16, tag="hs", name="hs")
            nc.sync.dma_start(
                out=t[:],
                in_=h[b, mc * MCH : (mc + 1) * MCH, :].rearrange("(p t) k -> p (t k)", t=4),
            )
            hs[(b, mc)] = t

        def load_mem(mc, ch):
            t = const.tile([P, 2048], BF16, name="mem%d_%d" % (mc, ch))
            nc.sync.dma_start(
                out=t[:].rearrange("p (t c) -> p t c", t=4),
                in_=memory[0, mc * MCH : (mc + 1) * MCH, ch * 512 : (ch + 1) * 512].rearrange(
                    "(p t) c -> p t c", t=4
                ),
            )
            mem[(mc, ch)] = t

        def load_x(b, ch):
            t = xstage.tile([P, 4096], BF16, tag="xs", name="xs")
            xv = x[b, :, ch * 512 : (ch + 1) * 512].rearrange("(p r) c -> p r c", r=8)
            tv = t[:].rearrange("p (r c) -> p r c", r=8)
            for i in range(2):
                nc.sync.dma_start(out=tv[:, 4 * i : 4 * i + 4, :], in_=xv[:, 4 * i : 4 * i + 4, :])
            xs[(b, ch)] = t

        loadq = [("h", 0, 0), ("w", 0, 0), ("b", 0, 0)] + [("h", b, 0) for b in range(1, LEAD + 1)] + [("m", 0, 0)]
        for b in range(NB):
            loadq += [("x", b, 0)]
            if b + LEAD + 1 < NB:
                loadq += [("h", b + LEAD + 1, 0)]
            elif b + LEAD + 1 - NB < H1_EARLY:
                loadq += [("h", b + LEAD + 1 - NB, 1)]
        h1rest = [("h", b, 1) for b in range(min(H1_EARLY, LEAD + 1), NB)]
        loadq += h1rest[:M1_POS] + [("m", 1, 0)] + h1rest[M1_POS:]
        loadq += [("w", 1, 0), ("m", 0, 1), ("m", 1, 1)] + [("x", b, 1) for b in range(NB)]
        st = {"next": 0, "x": 0, "h": 0}

        def pump():
            while st["next"] < len(loadq):
                kind, a0, a1 = loadq[st["next"]]
                if kind == "x" and st["x"] >= X_BUFS:
                    return
                if kind in ("h", "w") and st["h"] >= H_BUFS:
                    return
                if kind == "x":
                    load_x(a0, a1)
                    st["x"] += 1
                elif kind == "h":
                    load_h(a0, a1)
                    st["h"] += 1
                elif kind == "w":
                    load_w2(a0)
                    st["h"] += 1
                elif kind == "b":
                    nc.sync.dma_start(out=b2r[:], in_=b2.rearrange("(r c) -> r c", c=P))
                else:
                    load_mem(a0, a1)
                st["next"] += 1

        pump()

        w2c = [const.tile([P, 512], U32, name="w2c%d" % i, align_bytes=64) for i in range(2)]
        w2s = [const.tile([P, 512], U8, name="w2s%d" % i, align_bytes=64) for i in range(2)]

        def w2_regroup(q, eng):
            gw = grpp.tile([P, 1024], BF16, tag="grp", name="gw", align_bytes=64)
            dst = gw[:].rearrange("p (c t) -> p c t", t=4)
            src = w2raw[q // 2][:].rearrange("p (t c) -> p c t", t=4)[:, (q % 2) * 256 : (q % 2 + 1) * 256, :]
            if eng == "v":
                nc.vector.tensor_copy(out=dst, in_=src)
            elif eng == "g":
                nc.gpsimd.tensor_scalar(out=dst, in0=src, scalar1=1.0, scalar2=0.0, op0=ALU.mult, op1=ALU.add)
            else:
                nc.scalar.copy(out=dst, in_=src)
            return gw

        def w2_quant(q, gw):
            nc.vector.quantize_mx(
                out=w2c[q // 2][:, (q % 2) * 256 : (q % 2 + 1) * 256].bitcast(FP8X4),
                scales=w2s[q // 2][:, (q % 2) * 256 : (q % 2 + 1) * 256],
                in_=gw[:],
            )

        hc = {}
        hsc = {}

        def prep_pe(b, mc):
            hc[(b, mc)] = const.tile([P, MCH], U32, name="hc%d_%d" % (b, mc), align_bytes=64)
            hsc[(b, mc)] = const.tile([P, MCH], U8, name="hsc%d_%d" % (b, mc), align_bytes=64)
            hw = hs[(b, mc)][:].bitcast(F32)
            xts = []
            for half in range(2):
                xt = auxp.tile([P, 512], F32, tag="aux", name="xt")
                for ttl in range(2):
                    tt = 2 * half + ttl
                    for u in range(2):
                        nc.tensor.transpose(
                            xt[:, u * 256 + ttl * P : u * 256 + (ttl + 1) * P],
                            hw[:, tt * 256 + u * P : tt * 256 + (u + 1) * P],
                            ident[:],
                        )
                xts.append(xt)
            st["h"] -= 1
            pump()
            return (b, mc, xts)

        def prep_copy(job, half, eng):
            b, mc, xts = job
            gh = grpp.tile([P, 1024], BF16, tag="grp", name="gh", align_bytes=64)
            dst = gh[:].bitcast(F32).rearrange("p (c u) -> p c u", u=2)
            src = xts[half][:].rearrange("p (u c) -> p c u", u=2)
            if eng == "v":
                nc.vector.tensor_copy(out=dst, in_=src)
            else:
                nc.scalar.copy(out=dst, in_=src)
            return (b, mc, half, gh)

        def prep_h_back(pend):
            for b, mc, half, gh in pend:
                nc.vector.quantize_mx(
                    out=hc[(b, mc)][:, half * 256 : (half + 1) * 256].bitcast(FP8X4),
                    scales=hsc[(b, mc)][:, half * 256 : (half + 1) * 256],
                    in_=gh[:],
                )

        units = [(mc, ct) for mc in range(2) for ct in range(4)] + [(mc, ct) for ct in range(4, 8) for mc in range(2)]
        WIDE = [4, 5, 6]
        NU = len(units)
        gg = {}
        U = {}
        mT = {}
        Dt = {}
        ndone = {}

        def gkey(j, b):
            if j in NOPOOL:
                return ("n", j, b // 2), b % 2
            return (j // 2, b), j % 2

        def mx_sig(tiles):
            zs = []
            for j, b in tiles:
                mc, ct = units[j]
                z = auxp.tile([P, 512], F32, tag="aux", name="z")
                nc.tensor.matmul_mx(
                    out=z[:],
                    lhsT=w2c[ct // 4][:, (ct % 4) * P : (ct % 4 + 1) * P].bitcast(FP8X4),
                    lhsT_scale=w2s[ct // 4][:, (ct % 4) * P : (ct % 4 + 1) * P],
                    rhs=hc[(b, mc)][:].bitcast(FP8X4),
                    rhs_scale=hsc[(b, mc)][:],
                    start=True,
                    stop=True,
                )
                zs.append(z)
            for jb, z in zip(tiles, zs):
                ct = units[jb[0]][1]
                key, half = gkey(jb[0], jb[1])
                if key not in gg:
                    gg[key] = gp.tile([P, 1024], F32, tag="g", name="g")
                nc.scalar.activation(
                    out=gg[key][:, half * 512 : (half + 1) * 512],
                    in_=z[:],
                    func=ACT.Sigmoid,
                    bias=b2T[:, ct : ct + 1],
                    scale=1.0,
                )

        def memT_pe(k):
            t = auxp.tile([P, 1024], BF16, tag="aux", name="mT")
            for u in range(2):
                mc, ct = units[2 * k + u]
                for tt in range(4):
                    nc.tensor.transpose(
                        t[:, u * 512 + tt * P : u * 512 + (tt + 1) * P],
                        mem[(mc, ct // 4)][:, tt * 512 + (ct % 4) * P : tt * 512 + (ct % 4 + 1) * P],
                        identb[:],
                    )
            mT[k] = t

        def d_op(j, b):
            mc, ct = units[j]
            n = ndone.get(j, 0)
            if n % 2 == 0:
                Dt[(j, n // 2)] = dp.tile([P, 1024], F32, tag="d", name="d")
            nc.vector.scalar_tensor_tensor(
                out=Dt[(j, n // 2)][:, (n % 2) * 512 : (n % 2 + 1) * 512],
                in0=mT[j // 2][:, (j % 2) * 512 : (j % 2 + 1) * 512],
                scalar=U[(b, ct // 4)][:, ct % 4 : ct % 4 + 1],
                in1=gg[gkey(j, b)[0]][:, gkey(j, b)[1] * 512 : (gkey(j, b)[1] + 1) * 512],
                op0=ALU.subtract,
                op1=ALU.mult,
            )
            ndone[j] = n + 1
            if j not in NOPOOL and (n + 1) % 4 == 0:
                q = (n + 1) // 4 - 1
                for s in range(POOL_SPLIT):
                    wd = 1024 // POOL_SPLIT
                    nc.gpsimd.tensor_tensor(
                        out=Dt[(j, 2 * q)][:, s * wd : (s + 1) * wd],
                        in0=Dt[(j, 2 * q)][:, s * wd : (s + 1) * wd],
                        in1=Dt[(j, 2 * q + 1)][:, s * wd : (s + 1) * wd],
                        op=ALU.add,
                    )

        def d_wide(k, b):
            ct = units[2 * k][1]
            n = ndone.get(("w", k), 0)
            Dt[("w", k, n)] = dp.tile([P, 1024], F32, tag="d", name="d")
            nc.vector.scalar_tensor_tensor(
                out=Dt[("w", k, n)][:],
                in0=mT[k][:],
                scalar=U[(b, ct // 4)][:, ct % 4 : ct % 4 + 1],
                in1=gg[(k, b)][:],
                op0=ALU.subtract,
                op1=ALU.mult,
            )
            ndone[("w", k)] = n + 1
            if n % 2 == 1:
                nc.gpsimd.tensor_tensor(
                    out=Dt[("w", k, n - 1)][:], in0=Dt[("w", k, n - 1)][:], in1=Dt[("w", k, n)][:], op=ALU.add
                )

        def acc_wide(j):
            accs[j] = auxp.tile([P, 512], F32, tag="aux", name="acc")
            for q in range(4):
                for tt in range(4):
                    nc.tensor.matmul(
                        out=accs[j][:, tt * P : (tt + 1) * P],
                        lhsT=Dt[("w", j // 2, 2 * q)][:, (j % 2) * 512 + tt * P : (j % 2) * 512 + (tt + 1) * P],
                        rhs=ident[:],
                        is_transpose=True,
                        start=(q == 0 and tt == 0),
                        stop=(q == 3 and tt == 3),
                    )

        accs = {}
        ots = {}

        def acc_pe(j, parts):
            if parts[0] == 0:
                accs[j] = auxp.tile([P, 512], F32, tag="aux", name="acc")
            a = accs[j]
            lastp = 3 if j in NOPOOL else 2
            for i in parts:
                s = Dt[(j, i)]
                for half in range(2):
                    for tt in range(4):
                        nc.tensor.matmul(
                            out=a[:, tt * P : (tt + 1) * P],
                            lhsT=s[:, half * 512 + tt * P : half * 512 + (tt + 1) * P],
                            rhs=ident[:],
                            is_transpose=True,
                            start=(i == 0 and half == 0 and tt == 0),
                            stop=(i == lastp and half == 1 and tt == 3),
                        )

        def fin(j):
            mc, ct = units[j]
            ot = otp.tile([P, 512], F32, tag="ot", name="ot")
            nc.vector.scalar_tensor_tensor(
                out=ot[:].rearrange("p (t c) -> p t c", t=4),
                in0=accs[j][:].rearrange("p (t c) -> p t c", t=4),
                scalar=-0.125,
                in1=mem[(mc, ct // 4)][:].rearrange("p (t c) -> p t c", t=4)[
                    :, :, (ct % 4) * P : (ct % 4 + 1) * P
                ],
                op0=ALU.mult,
                op1=ALU.add,
            )
            ots[j] = ot

        def store(j):
            mc, ct = units[j]
            nc.sync.dma_start(
                out=out[0, mc * MCH : (mc + 1) * MCH, ct * P : (ct + 1) * P].rearrange(
                    "(p t) c -> p t c", t=4
                ),
                in_=ots[j][:].rearrange("p (t c) -> p t c", t=4),
            )

        xps = {}

        def xmean_pe(b, ch):
            ps = auxp.tile([P, 512], F32, tag="aux", name="xps")
            for c4 in range(4):
                for r in range(8):
                    nc.tensor.matmul(
                        out=ps[:, c4 * 2 : c4 * 2 + 2],
                        lhsT=xs[(b, ch)][:, r * 512 + c4 * P : r * 512 + (c4 + 1) * P],
                        rhs=ones[:],
                        start=(r == 0),
                        stop=(r == 7),
                    )
            xps[(b, ch)] = ps
            st["x"] -= 1
            pump()

        def xmean_out(b, ch):
            ub = const.tile([P, 4], F32, name="U%d_%d" % (b, ch))
            nc.vector.tensor_copy(
                out=ub[:], in_=xps[(b, ch)][:, 0:8].rearrange("p (c two) -> p c two", two=2)[:, :, 0]
            )
            U[(b, ch)] = ub

        gw0 = w2_regroup(0, "v")
        gw1 = w2_regroup(1, "s")
        st["h"] -= 1
        pump()
        nc.vector.tensor_copy(out=bzf[0:8, :], in_=b2r[:])
        b2ps = auxp.tile([P, 512], F32, tag="aux", name="b2ps")
        nc.tensor.transpose(b2ps[:, 0:P], bzf[:], ident[:])
        b2T = const.tile([P, 8], F32, name="b2T")
        w2_quant(0, gw0)
        nc.vector.tensor_copy(out=b2T[:], in_=b2ps[:, 0:8])
        w2_quant(1, gw1)

        rounds = [[(j, b) for j in range(4)] for b in range(NB)]
        first_round = {0: 0, 1: 0}
        k0 = 2
        if PH2_G4:
            rounds += [[] for i in range(GAP)]
            first_round[2] = NB + GAP
            first_round[3] = NB + GAP
            rounds += [[(j, b) for j in range(4, 8)] for b in range(NB)]
            k0 = 4
        for k in range(k0, NU // 2):
            first_round[k] = len(rounds)
            if k == NU // 2 - 1:
                for j in (2 * k, 2 * k + 1):
                    rounds.append([(j, b) for b in range(4)])
                    rounds.append([(j, b) for b in range(4, 8)])
            else:
                for bb in range(0, NB, 2):
                    rounds.append([(2 * k, bb), (2 * k + 1, bb), (2 * k, bb + 1), (2 * k + 1, bb + 1)])
        NR = len(rounds)
        prep_at = {}
        for b in range(NB):
            prep_at.setdefault(b - LEAD, []).append((b, 0))
            if PH2_G4:
                prep_at.setdefault(NB + GAP + b - LEAD, []).append((b, 1))
            else:
                prep_at.setdefault(H1_BASE + b // 2, []).append((b, 1))
        xrel = {}
        for b in range(NB):
            xrel.setdefault(b + X0_BASE, []).append((b, 0))
            xrel.setdefault(X1_BASE + GAP + (6 * b) // 7, []).append((b, 1))

        made = []
        released = []
        store_wait = []
        part_wait = []
        acc_wait = []
        fin_wait = []
        xout_wait = []
        copy_wait = []
        quant_wait = []

        for r in range(-LEAD, NR + 12):
            new_quant = []
            for job in copy_wait:
                engs = (H0_COPY if job[1] == 0 else H1_COPY)[job[0] % 2]
                new_quant.append(prep_copy(job, 0, engs[0]))
                new_quant.append(prep_copy(job, 1, engs[1]))
            if 0 <= r < NR:
                mx_sig(rounds[r])
            new_copy = []
            new_xout = []
            if XFIRST:
                for b, ch in xrel.get(r, []):
                    xmean_pe(b, ch)
                    new_xout.append((b, ch))
            for b, mc in prep_at.get(r, []):
                new_copy.append(prep_pe(b, mc))
            if not XFIRST:
                for b, ch in xrel.get(r, []):
                    xmean_pe(b, ch)
                    new_xout.append((b, ch))
            now_acc = [j for rr, j in acc_wait if rr + (ACC_LAG_W if j // 2 in WIDE else ACC_LAG) <= r][:ACC_PER_STEP]
            acc_wait = [e for e in acc_wait if e[1] not in now_acc]
            for j in now_acc:
                if j // 2 in WIDE:
                    acc_wide(j)
                else:
                    acc_pe(j, [0, 2])
            for j, i in part_wait:
                acc_pe(j, [i])
                if i == 3:
                    now_acc.append(j)
            part_wait = []
            for k in range(NU // 2):
                if first_round[k] - MT_LEAD == r:
                    memT_pe(k)
            copy_wait = new_copy
            for b, ch in xout_wait:
                xmean_out(b, ch)
                released.append((b, ch))
            xout_wait = new_xout
            for rr, j in store_wait:
                if rr + (STORE_LAG if r < NR else 0) <= r:
                    store(j)
            store_wait = [e for e in store_wait if e[0] + (STORE_LAG if r < NR else 0) > r]
            for j in fin_wait:
                fin(j)
                if r >= NR:
                    store(j)
                else:
                    store_wait.append((r, j))
            fin_wait = now_acc
            if r == W2_STEP:
                gw2 = w2_regroup(2, W2_ENG)
                gw3 = w2_regroup(3, W2_ENG)
                st["h"] -= 1
                pump()
            if r == W2_STEP + 1:
                w2_quant(2, gw2)
                w2_quant(3, gw3)
            if 1 <= r <= NR:
                made += [jb for jb in rounds[r - 1] if jb[0] // 2 not in WIDE or jb[0] % 2 == 1]
            taken = 0
            while made and taken < D_QUOTA:
                j, b = made[0]
                if (b, units[j][1] // 4) not in released:
                    break
                made = made[1:]
                if j // 2 in WIDE:
                    d_wide(j // 2, b)
                    taken += 2
                    if ndone[("w", j // 2)] == NB:
                        acc_wait.append((r, j - 1))
                        acc_wait.append((r, j))
                    continue
                d_op(j, b)
                taken += 1
                if j in NOPOOL:
                    if ndone[j] % 2 == 0:
                        part_wait.append((j, ndone[j] // 2 - 1))
                elif ndone[j] == NB:
                    acc_wait.append((r, j))
            prep_h_back(new_quant)
